import numpy as np
import ml_dtypes


def mxq(x, axis, fmt="e4m3"):
    dtype, down = {"e4m3": (ml_dtypes.float8_e4m3fn, 7), "e5m2": (ml_dtypes.float8_e5m2, 14)}[fmt]
    v = np.moveaxis(np.asarray(x, np.float32).astype(ml_dtypes.bfloat16).astype(np.float64), axis, -1)
    blocks = v.reshape(v.shape[:-1] + (-1, 32))
    amax = np.abs(blocks).max(-1, keepdims=True)
    byte = np.maximum(np.where(amax > 0, np.frexp(amax)[1] - 1 + 127, 0) - down, 1)
    scale = np.exp2(byte - 127.0)
    codes = (blocks / scale).astype(np.float32).astype(dtype).astype(np.float64)
    return np.moveaxis((codes * scale).reshape(v.shape), -1, axis)


WIDE = False


def mx_kscale(k):
    if not WIDE:
        return np.ones(k)
    levels = np.array([10, -10, 5, -5, 0])
    if k % 512:
        return np.exp2(np.random.permutation(np.resize(levels, k // 32))).repeat(32)
    a = np.empty((k // 512, 16))
    for p in range(k // 512):
        a[p, :8] = np.random.permutation(np.resize(levels, 8))
        for g in range(8):
            far = levels[np.abs(levels - a[p, g]) >= 10]
            a[p, g + 8] = far[np.random.randint(len(far))]
    return np.exp2(a.ravel()).repeat(32)


BF16 = ml_dtypes.bfloat16


def bf(x):
    return np.asarray(x, np.float32).astype(BF16)


def f64(x):
    return np.asarray(x).astype(np.float64)


B, N, M, A, P, W = 8, 1024, 4, 32, 4, 32


def normalize(adj):
    mx = adj + np.eye(N)[None, :, :]
    rowsum = mx.sum(axis=2)
    r_inv = 1.0 / rowsum
    r_inv = np.where(np.isinf(r_inv), 0.0, r_inv)
    return mx * r_inv[:, :, None]


def setup_inputs():
    bound = 0.5 * np.sqrt(3.0 * N / (M * A))
    s = mx_kscale(N)
    t = s / s.min()
    g = 2.0 ** np.round(np.log2(t.mean()))
    return {"x": bf(np.random.standard_normal((B, N, M, A)) * (g / t)[None, :, None, None]),
            "adj": bf(np.random.uniform(0.0, 1.0, (B, N, N)) * (4.0 / np.sqrt(N)) * t[None, None, :]),
            "weight": bf(np.random.uniform(-bound, bound, (M, P, A, W))),
            "bias": bf(np.random.uniform(0.0, 1.0, (1, 1, P, W)))}


def reference(x, adj, weight, bias):
    h = f64(x).reshape(B, N, M * A) @ f64(weight).transpose(0, 2, 1, 3).reshape(M * A, P * W)
    adj_n = normalize(f64(adj))
    agg = mxq(adj_n, 2, "e4m3") @ mxq(h, 1, "e4m3")
    return np.maximum(agg, 0.0).reshape(B, N, P, W) + f64(bias)

@@ -1,0 +1,303 @@
+from contextlib import ExitStack
+
+import concourse.mybir as mybir
+from concourse.masks import make_identity
+
+BF16 = mybir.dt.bfloat16
+F32 = mybir.dt.float32
+U32 = mybir.dt.uint32
+U8 = mybir.dt.uint8
+FP8X4 = mybir.dt.float8_e4m3fn_x4
+ALU = mybir.AluOpType
+ACT = mybir.ActivationFunctionType
+
+B = 8
+N = 1024
+F = 128
+P = 128
+NB = N // P
+ROWS = B * NB
+PASSES = N // (4 * P)
+FLOPS = 2 * B * N * N * F + 2 * B * N * F * F
+
+VECTOR_SUMS = 6
+GROUP_SIZES = [4] * (ROWS // 4 - 1) + [2, 1, 1]
+LAG_TRANSPOSE = 1
+LAG_COPY = 2
+LAG_QUANTISE = 4
+LAG_MATMUL = 6
+LAG_OUTPUT = 8
+
+
+def tile_spconvlayer_kernel(tc, x, adj, weight, bias, out):
+    nc = tc.nc
+    with ExitStack() as ctx:
+        const = ctx.enter_context(tc.tile_pool(name="const", bufs=1))
+        adj_pool = ctx.enter_context(tc.tile_pool(name="adj_pool", bufs=4))
+        norm_pool = ctx.enter_context(tc.tile_pool(name="norm_pool", bufs=3))
+        scaled_pool = ctx.enter_context(tc.tile_pool(name="scaled_pool", bufs=6))
+        group_pool = ctx.enter_context(tc.tile_pool(name="group_pool", bufs=3))
+        h_pool = ctx.enter_context(tc.tile_pool(name="h_pool", bufs=3))
+        turn_psum = ctx.enter_context(tc.psum_pool(name="turn_psum", bufs=6))
+        product_psum = ctx.enter_context(tc.psum_pool(name="product_psum", bufs=2))
+        ctx.enter_context(tc.manual_schedule())
+
+        x_view = x.rearrange("b (g p t) m a -> b p g (t m a)", p=P, t=4)
+        adj_view = adj.rearrange("b (nb p) c -> b p nb c", p=P)
+        out_view = out.rearrange("b (nb p) u w -> b p nb (u w)", p=P)
+
+        identity = const.tile([P, P], BF16)
+        make_identity(nc, identity[:])
+        w_sb = const.tile([P, F], BF16)
+        for m in range(4):
+            nc.scalar.dma_start(
+                out=w_sb[32 * m : 32 * m + 32, :].rearrange("a (u w) -> a u w", u=4),
+                in_=weight[m].rearrange("u a w -> a u w"),
+            )
+        bias_bf16 = const.tile([P, F], BF16)
+        nc.scalar.dma_start(
+            out=bias_bf16[:], in_=bias.rearrange("o i u w -> (o i u w)").partition_broadcast(P)
+        )
+        bias_f32 = const.tile([P, F], F32)
+        x_sb = const.tile([P, B, PASSES, 4 * F], BF16)
+        h_codes = const.tile([P, B * PASSES * F], U32, align_bytes=64)
+        h_scales = const.tile([P, B * PASSES * F], U8, align_bytes=64)
+        unused_vector = const.tile([P, N], BF16)
+        unused_scalar = const.tile([P, N], BF16)
+
+        adj_sb = {}
+        sums = {}
+        r = {}
+        with_loops = {}
+        x_turned = {}
+        h_grouped = {}
+        scaled = {}
+        turned = {}
+        grouped = {}
+        codes = {}
+        scales = {}
+        product = {}
+
+        first_row = [sum(GROUP_SIZES[:u]) for u in range(len(GROUP_SIZES))]
+        group_of = {}
+        for u in range(len(GROUP_SIZES)):
+            for q in range(GROUP_SIZES[u]):
+                group_of[first_row[u] + q] = u
+
+        def ends_group(i):
+            return 0 <= i < ROWS and group_of.get(i + 1, -1) != group_of[i]
+
+        def load_adj(b, lo, hi):
+            if b not in adj_sb:
+                adj_sb[b] = adj_pool.tile([P, (NB + 1) * N], BF16, name="adj_sb")
+            rows = adj_sb[b][:, 0 : NB * N].rearrange("p (nb c) -> p nb c", c=N)
+            nc.sync.dma_start(out=rows[:, lo:hi, :], in_=adj_view[b][:, lo:hi, :])
+
+        def load_x(b):
+            nc.sync.dma_start(out=x_sb[:, b, :, :], in_=x_view[b])
+
+        def column(nb):
+            return nb + 8 - VECTOR_SUMS
+
+        def sum_rows(b, nb):
+            if b not in sums:
+                sums[b] = norm_pool.tile([P, 16], F32, name="sums")
+            rows = adj_sb[b][:, nb * N : (nb + 1) * N]
+            total = sums[b][:, column(nb) : column(nb) + 1]
+            if nb < VECTOR_SUMS:
+                nc.vector.tensor_scalar(
+                    out=unused_vector[:],
+                    in0=rows,
+                    scalar1=1.0,
+                    scalar2=1.0,
+                    op0=ALU.mult,
+                    op1=ALU.add,
+                    accum_out=total,
+                )
+            else:
+                nc.scalar.activation(
+                    out=unused_scalar[:], in_=rows, func=ACT.Copy, bias=1.0 / N, accum_out=total
+                )
+
+        def add_self_loops(b, lo, hi):
+            if b not in with_loops:
+                with_loops[b] = norm_pool.tile([P, NB, P], F32, name="with_loops")
+            nc.vector.tensor_tensor(
+                out=with_loops[b][:, lo:hi, :],
+                in0=adj_sb[b][:].rearrange("p (nb c) -> p nb c", c=N + P)[:, lo:hi, 0:P],
+                in1=identity[:].unsqueeze(1).to_broadcast([P, hi - lo, P]),
+                op=ALU.add,
+            )
+
+        def invert_sums(b, lo, hi):
+            if b not in r:
+                r[b] = norm_pool.tile([P, 16], F32, name="r")
+            nc.vector.reciprocal(r[b][:, column(lo) : column(hi)], sums[b][:, column(lo) : column(hi)])
+
+        def scale_rows(i):
+            b, nb = divmod(i, NB)
+            scaled[i] = scaled_pool.tile([P, N], BF16, name="scaled")
+            row = adj_sb[b][:, nb * N : (nb + 1) * N]
+            lo, hi = nb * P, (nb + 1) * P
+            pieces = [(lo, hi, with_loops[b][:, nb, :])]
+            if lo > 0:
+                pieces.append((0, lo, row[:, 0:lo]))
+            if hi < N:
+                pieces.append((hi, N, row[:, hi:N]))
+            for first, last, source in pieces:
+                nc.vector.tensor_scalar(
+                    out=scaled[i][:, first:last],
+                    in0=source,
+                    scalar1=r[b][:, column(nb) : column(nb) + 1],
+                    scalar2=None,
+                    op0=ALU.mult,
+                )
+
+        def transpose_rows(i):
+            turned[i] = turn_psum.tile([P, PASSES, 4, P], BF16, tag="turn", name="turned")
+            for block in range(NB):
+                g, t = divmod(block, 4)
+                source = scaled[i][:, 4 * P * g + t : 4 * P * (g + 1) : 4]
+                nc.tensor.transpose(turned[i][:, g, t, :], source, identity[:])
+
+        def copy_rows(i):
+            u = group_of[i]
+            q = i - first_row[u]
+            if q == 0:
+                grouped[u] = group_pool.tile([P, GROUP_SIZES[u] * N], BF16, align_bytes=64, name="grouped")
+            nc.scalar.copy(
+                out=grouped[u][:, q * N : (q + 1) * N].rearrange("p (g n t) -> p g n t", g=PASSES, t=4),
+                in_=turned[i][:].rearrange("p g t n -> p g n t"),
+            )
+
+        def quantise_group(u):
+            width = GROUP_SIZES[u] * PASSES * P
+            codes[u] = group_pool.tile([P, width], U32, align_bytes=64, name="codes")
+            scales[u] = group_pool.tile([P, width], U8, align_bytes=64, name="scales")
+            nc.vector.quantize_mx(out=codes[u][:].bitcast(FP8X4), scales=scales[u][:], in_=grouped[u][:])
+
+        def multiply_group(u):
+            b = first_row[u] // NB
+            product[u] = product_psum.tile([P, GROUP_SIZES[u], F], F32, name="product")
+            for q in range(GROUP_SIZES[u]):
+                for g in range(PASSES):
+                    a_cols = slice((q * PASSES + g) * P, (q * PASSES + g + 1) * P)
+                    h_cols = slice((b * PASSES + g) * F, (b * PASSES + g + 1) * F)
+                    nc.tensor.matmul_mx(
+                        out=product[u][:, q, :],
+                        lhsT=codes[u][:, a_cols].bitcast(FP8X4),
+                        lhsT_scale=scales[u][:, a_cols],
+                        rhs=h_codes[:, h_cols].bitcast(FP8X4),
+                        rhs_scale=h_scales[:, h_cols],
+                        start=(g == 0),
+                        stop=(g == PASSES - 1),
+                    )
+
+        def output_group(u):
+            b, nb = divmod(first_row[u], NB)
+            size = GROUP_SIZES[u]
+            result = group_pool.tile([P, size, F], F32, name="result")
+            nc.vector.scalar_tensor_tensor(
+                out=result[:],
+                in0=product[u][:],
+                scalar=0.0,
+                in1=bias_f32[:].unsqueeze(1).to_broadcast([P, size, F]),
+                op0=ALU.max,
+                op1=ALU.add,
+            )
+            nc.sync.dma_start(out=out_view[b][:, nb : nb + size, :], in_=result[:])
+
+        def transpose_x(b):
+            bank = turn_psum.tile([P, NB, P], BF16, tag="turn", name="x_bank")
+            for j in range(NB):
+                nc.tensor.transpose(bank[:, j, :], x_sb[:, b, j // 4, (j % 4) * F : (j % 4 + 1) * F], identity[:])
+            x_turned[b] = h_pool.tile([P, NB, P], BF16, name="x_turned")
+            nc.scalar.copy(out=x_turned[b][:], in_=bank[:])
+
+        def multiply_x(b):
+            h_grouped[b] = h_pool.tile([P, PASSES, F, 4], BF16, align_bytes=64, name="h_grouped")
+            for g in range(PASSES):
+                bank = turn_psum.tile([P, 4, F], F32, tag="turn", name="h_bank")
+                for t in range(4):
+                    nc.tensor.matmul(
+                        bank[:, t, :], lhsT=x_turned[b][:, 4 * g + t, :], rhs=w_sb[:], start=True, stop=True
+                    )
+                nc.scalar.copy(out=h_grouped[b][:, g, :, :], in_=bank[:].rearrange("p t f -> p f t"))
+
+        def quantise_h(b):
+            cols = slice(b * PASSES * F, (b + 1) * PASSES * F)
+            nc.vector.quantize_mx(
+                out=h_codes[:, cols].bitcast(FP8X4),
+                scales=h_scales[:, cols],
+                in_=h_grouped[b][:].rearrange("p g f t -> p (g f t)"),
+            )
+
+        load_adj(0, 0, 1)
+        load_adj(0, 1, 2)
+        load_x(0)
+        load_adj(0, 2, 3)
+        load_adj(0, 3, 4)
+        load_x(1)
+        load_adj(0, 4, 6)
+        load_adj(0, 6, 8)
+        load_adj(1, 0, 2)
+        load_adj(1, 2, 4)
+        load_x(2)
+        load_adj(1, 4, 6)
+        load_adj(1, 6, 8)
+        for b in range(3, B):
+            load_x(b)
+        for b in range(2, 4):
+            load_adj(b, 0, 4)
+            load_adj(b, 4, 8)
+
+        half = NB // 2
+        for nb in range(half):
+            sum_rows(0, nb)
+        add_self_loops(0, 0, half)
+        invert_sums(0, 0, half)
+        transpose_x(0)
+
+        for step in range(ROWS + LAG_OUTPUT + 1):
+            b, k = divmod(step, NB)
+            following = b + 1
+            if following < B and k == 7:
+                invert_sums(following, 0, NB)
+            if step < ROWS:
+                scale_rows(step)
+            if step < 2:
+                sum_rows(0, half + step)
+            if step == 2:
+                add_self_loops(0, half, NB)
+                invert_sums(0, half, NB)
+                nc.vector.tensor_copy(out=bias_f32[:], in_=bias_bf16[:])
+            if following < B:
+                if k < VECTOR_SUMS:
+                    sum_rows(following, k)
+                if k == 6:
+                    add_self_loops(following, 0, NB)
+            if k == 7 and b + 4 < B:
+                load_adj(b + 4, 0, half)
+                load_adj(b + 4, half, NB)
+            if 0 <= step - LAG_TRANSPOSE < ROWS:
+                transpose_rows(step - LAG_TRANSPOSE)
+            if 0 <= step - LAG_COPY < ROWS:
+                copy_rows(step - LAG_COPY)
+            j, odd = divmod(step, 2)
+            if not odd and j < B:
+                multiply_x(j)
+            if odd and j + 1 < B:
+                transpose_x(j + 1)
+            if odd and 0 <= j - 1 < B:
+                quantise_h(j - 1)
+            if step == 0:
+                sum_rows(0, VECTOR_SUMS)
+                sum_rows(0, VECTOR_SUMS + 1)
+            if following < B and k in (2, 4):
+                sum_rows(following, VECTOR_SUMS + k // 2 - 1)
+            if ends_group(step - LAG_QUANTISE):
+                quantise_group(group_of[step - LAG_QUANTISE])
+            if ends_group(step - LAG_MATMUL):
+                multiply_group(group_of[step - LAG_MATMUL])
+            if ends_group(step - LAG_OUTPUT):
+                output_group(group_of[step - LAG_OUTPUT])

@@ -48,6 +48,8 @@ def tile_spconvlayer_kernel(tc, x, adj, weight, bias, out):
 
         identity = const.tile([P, P], BF16)
         make_identity(nc, identity[:])
+        identity_f32 = const.tile([P, P], F32)
+        make_identity(nc, identity_f32[:])
         w_sb = const.tile([P, F], BF16)
         for m in range(4):
             nc.scalar.dma_start(
@@ -154,11 +156,12 @@ def tile_spconvlayer_kernel(tc, x, adj, weight, bias, out):
                 )
 
         def transpose_rows(i):
-            turned[i] = turn_psum.tile([P, PASSES, 4, P], BF16, tag="turn", name="turned")
-            for block in range(NB):
-                g, t = divmod(block, 4)
-                source = scaled[i][:, 4 * P * g + t : 4 * P * (g + 1) : 4]
-                nc.tensor.transpose(turned[i][:, g, t, :], source, identity[:])
+            turned[i] = turn_psum.tile([P, PASSES, 2, P], F32, tag="turn", name="turned")
+            words = scaled[i][:].bitcast(F32)
+            for g in range(PASSES):
+                for u in range(2):
+                    source = words[:, 2 * P * g + u : 2 * P * (g + 1) : 2]
+                    nc.tensor.transpose(turned[i][:, g, u, :], source, identity_f32[:])
 
         def copy_rows(i):
             u = group_of[i]
@@ -166,8 +169,8 @@ def tile_spconvlayer_kernel(tc, x, adj, weight, bias, out):
             if q == 0:
                 grouped[u] = group_pool.tile([P, GROUP_SIZES[u] * N], BF16, align_bytes=64, name="grouped")
             nc.scalar.copy(
-                out=grouped[u][:, q * N : (q + 1) * N].rearrange("p (g n t) -> p g n t", g=PASSES, t=4),
-                in_=turned[i][:].rearrange("p g t n -> p g n t"),
+                out=grouped[u][:, q * N : (q + 1) * N].bitcast(F32).rearrange("p (g n e) -> p g n e", g=PASSES, e=2),
+                in_=turned[i][:].rearrange("p g e n -> p g n e"),
             )
 
         def quantise_group(u):

@@ -20,12 +20,16 @@ ROWS = B * NB
 PASSES = N // (4 * P)
 FLOPS = 2 * B * N * N * F + 2 * B * N * F * F
 
-VECTOR_SUMS = 6
+HALF = 4
+HALVES = ROWS // HALF
+ADJ_BUFS = 12
 GROUP_SIZES = [4] * (ROWS // 4 - 1) + [2, 1, 1]
-LAG_TRANSPOSE = 1
-LAG_COPY = 2
-LAG_QUANTISE = 4
-LAG_MATMUL = 6
+LEAD_SUM = 6
+LAG_DIAGONAL = 1
+LAG_TRANSPOSE = 2
+LAG_COPY = 3
+LAG_QUANTISE = 6
+LAG_MATMUL = 7
 LAG_OUTPUT = 8
 
 
@@ -33,33 +37,32 @@ def tile_spconvlayer_kernel(tc, x, adj, weight, bias, out):
     nc = tc.nc
     with ExitStack() as ctx:
         const = ctx.enter_context(tc.tile_pool(name="const", bufs=1))
-        adj_pool = ctx.enter_context(tc.tile_pool(name="adj_pool", bufs=4))
+        adj_pool = ctx.enter_context(tc.tile_pool(name="adj_pool", bufs=ADJ_BUFS))
         norm_pool = ctx.enter_context(tc.tile_pool(name="norm_pool", bufs=3))
         scaled_pool = ctx.enter_context(tc.tile_pool(name="scaled_pool", bufs=6))
         group_pool = ctx.enter_context(tc.tile_pool(name="group_pool", bufs=3))
-        h_pool = ctx.enter_context(tc.tile_pool(name="h_pool", bufs=3))
+        h_pool = ctx.enter_context(tc.tile_pool(name="h_pool", bufs=2))
         turn_psum = ctx.enter_context(tc.psum_pool(name="turn_psum", bufs=6))
         product_psum = ctx.enter_context(tc.psum_pool(name="product_psum", bufs=2))
         ctx.enter_context(tc.manual_schedule())
 
         x_view = x.rearrange("b (g p t) m a -> b p g (t m a)", p=P, t=4)
-        adj_view = adj.rearrange("b (nb p) c -> b p nb c", p=P)
+        adj_view = adj.rearrange("b (half q p) c -> (b half) p q c", p=P, q=HALF)
         out_view = out.rearrange("b (nb p) u w -> b p nb (u w)", p=P)
+
+        warm = const.tile([P, 2], F32)
+        nc.vector.memset(warm[:], 0.0)
+        nc.scalar.activation(out=warm[:, 0:1], in_=warm[:, 1:2], func=ACT.Copy)
 
         identity = const.tile([P, P], BF16)
         make_identity(nc, identity[:])
         identity_f32 = const.tile([P, P], F32)
         make_identity(nc, identity_f32[:])
+        ones = const.tile([P, P], BF16)
+        nc.gpsimd.memset(ones[:], 1.0)
+        bias_row = const.tile([P, F], BF16)
+        nc.gpsimd.memset(bias_row[:], 0.0)
         w_sb = const.tile([P, F], BF16)
-        for m in range(4):
-            nc.scalar.dma_start(
-                out=w_sb[32 * m : 32 * m + 32, :].rearrange("a (u w) -> a u w", u=4),
-                in_=weight[m].rearrange("u a w -> a u w"),
-            )
-        bias_bf16 = const.tile([P, F], BF16)
-        nc.scalar.dma_start(
-            out=bias_bf16[:], in_=bias.rearrange("o i u w -> (o i u w)").partition_broadcast(P)
-        )
         bias_f32 = const.tile([P, F], F32)
         x_sb = const.tile([P, B, PASSES, 4 * F], BF16)
         h_codes = const.tile([P, B * PASSES * F], U32, align_bytes=64)
@@ -89,27 +92,41 @@ def tile_spconvlayer_kernel(tc, x, adj, weight, bias, out):
         def ends_group(i):
             return 0 <= i < ROWS and group_of.get(i + 1, -1) != group_of[i]
 
-        def load_adj(b, lo, hi):
-            if b not in adj_sb:
-                adj_sb[b] = adj_pool.tile([P, (NB + 1) * N], BF16, name="adj_sb")
-            rows = adj_sb[b][:, 0 : NB * N].rearrange("p (nb c) -> p nb c", c=N)
-            nc.sync.dma_start(out=rows[:, lo:hi, :], in_=adj_view[b][:, lo:hi, :])
+        def load_adj(half, lo, hi):
+            if half not in adj_sb:
+                adj_sb[half] = adj_pool.tile([P, (HALF + 1) * N], BF16, name="adj_sb")
+            rows = adj_sb[half][:, 0 : HALF * N].rearrange("p (q c) -> p q c", c=N)
+            nc.sync.dma_start(out=rows[:, lo:hi, :], in_=adj_view[half][:, lo:hi, :])
 
         def load_x(b):
             nc.sync.dma_start(out=x_sb[:, b, :, :], in_=x_view[b])
 
-        def column(nb):
-            return nb + 8 - VECTOR_SUMS
+        def load_constants():
+            for m in range(4):
+                nc.sync.dma_start(
+                    out=w_sb[32 * m : 32 * m + 32, :].rearrange("a (u w) -> a u w", u=4),
+                    in_=weight[m].rearrange("u a w -> a u w"),
+                )
+            nc.sync.dma_start(out=bias_row[0:1, :], in_=bias.rearrange("o i u w -> (o i) (u w)"))
 
-        def sum_rows(b, nb):
-            if b not in sums:
-                sums[b] = norm_pool.tile([P, 16], F32, name="sums")
-            rows = adj_sb[b][:, nb * N : (nb + 1) * N]
-            total = sums[b][:, column(nb) : column(nb) + 1]
-            if nb < VECTOR_SUMS:
+        def spread_bias():
+            bank = turn_psum.tile([P, F], F32, tag="turn", name="bias_bank")
+            nc.tensor.matmul(bank[:], lhsT=ones[:], rhs=bias_row[:], start=True, stop=True)
+            nc.scalar.copy(out=bias_f32[:], in_=bank[:])
+
+        def row(i):
+            half, q = divmod(i, HALF)
+            return adj_sb[half][:, q * N : (q + 1) * N]
+
+        def sum_rows(i):
+            half, q = divmod(i, HALF)
+            if half not in sums:
+                sums[half] = norm_pool.tile([P, HALF], F32, name="sums")
+            total = sums[half][:, q : q + 1]
+            if i % 2 == 0 and i != 4 or i == 3:
                 nc.vector.tensor_scalar(
                     out=unused_vector[:],
-                    in0=rows,
+                    in0=row(i),
                     scalar1=1.0,
                     scalar2=1.0,
                     op0=ALU.mult,
@@ -118,50 +135,49 @@ def tile_spconvlayer_kernel(tc, x, adj, weight, bias, out):
                 )
             else:
                 nc.scalar.activation(
-                    out=unused_scalar[:], in_=rows, func=ACT.Copy, bias=1.0 / N, accum_out=total
+                    out=unused_scalar[:], in_=row(i), func=ACT.Copy, bias=1.0 / N, accum_out=total
                 )
 
-        def add_self_loops(b, lo, hi):
-            if b not in with_loops:
-                with_loops[b] = norm_pool.tile([P, NB, P], F32, name="with_loops")
+        def add_self_loops(half):
+            start = half % 2 * HALF * P
+            blocks = adj_sb[half][:, start : start + HALF * (N + P)].rearrange("p (q c) -> p q c", c=N + P)
+            with_loops[half] = norm_pool.tile([P, HALF, P], F32, name="with_loops")
             nc.vector.tensor_tensor(
-                out=with_loops[b][:, lo:hi, :],
-                in0=adj_sb[b][:].rearrange("p (nb c) -> p nb c", c=N + P)[:, lo:hi, 0:P],
-                in1=identity[:].unsqueeze(1).to_broadcast([P, hi - lo, P]),
+                out=with_loops[half][:],
+                in0=blocks[:, :, 0:P],
+                in1=identity[:].unsqueeze(1).to_broadcast([P, HALF, P]),
                 op=ALU.add,
             )
 
-        def invert_sums(b, lo, hi):
-            if b not in r:
-                r[b] = norm_pool.tile([P, 16], F32, name="r")
-            nc.vector.reciprocal(r[b][:, column(lo) : column(hi)], sums[b][:, column(lo) : column(hi)])
+        def invert_sums(half):
+            r[half] = norm_pool.tile([P, HALF], F32, name="r")
+            nc.vector.reciprocal(r[half][:], sums[half][:])
 
         def scale_rows(i):
-            b, nb = divmod(i, NB)
+            half, q = divmod(i, HALF)
             scaled[i] = scaled_pool.tile([P, N], BF16, name="scaled")
-            row = adj_sb[b][:, nb * N : (nb + 1) * N]
-            lo, hi = nb * P, (nb + 1) * P
-            pieces = [(lo, hi, with_loops[b][:, nb, :])]
-            if lo > 0:
-                pieces.append((0, lo, row[:, 0:lo]))
-            if hi < N:
-                pieces.append((hi, N, row[:, hi:N]))
-            for first, last, source in pieces:
-                nc.vector.tensor_scalar(
-                    out=scaled[i][:, first:last],
-                    in0=source,
-                    scalar1=r[b][:, column(nb) : column(nb) + 1],
-                    scalar2=None,
-                    op0=ALU.mult,
-                )
+            nc.vector.tensor_scalar(
+                out=scaled[i][:], in0=row(i), scalar1=r[half][:, q : q + 1], scalar2=None, op0=ALU.mult
+            )
+
+        def scale_diagonal(i):
+            half, q = divmod(i, HALF)
+            nb = i % NB
+            nc.vector.tensor_scalar(
+                out=scaled[i][:, nb * P : (nb + 1) * P],
+                in0=with_loops[half][:, q, :],
+                scalar1=r[half][:, q : q + 1],
+                scalar2=None,
+                op0=ALU.mult,
+            )
 
         def transpose_rows(i):
             turned[i] = turn_psum.tile([P, PASSES, 2, P], F32, tag="turn", name="turned")
-            words = scaled[i][:].bitcast(F32)
+            pairs = scaled[i][:].bitcast(F32)
             for g in range(PASSES):
-                for u in range(2):
-                    source = words[:, 2 * P * g + u : 2 * P * (g + 1) : 2]
-                    nc.tensor.transpose(turned[i][:, g, u, :], source, identity_f32[:])
+                for e in range(2):
+                    source = pairs[:, 2 * P * g + e : 2 * P * (g + 1) : 2]
+                    nc.tensor.transpose(turned[i][:, g, e, :], source, identity_f32[:])
 
         def copy_rows(i):
             u = group_of[i]
@@ -217,15 +233,15 @@ def tile_spconvlayer_kernel(tc, x, adj, weight, bias, out):
             x_turned[b] = h_pool.tile([P, NB, P], BF16, name="x_turned")
             nc.scalar.copy(out=x_turned[b][:], in_=bank[:])
 
-        def multiply_x(b):
-            h_grouped[b] = h_pool.tile([P, PASSES, F, 4], BF16, align_bytes=64, name="h_grouped")
-            for g in range(PASSES):
-                bank = turn_psum.tile([P, 4, F], F32, tag="turn", name="h_bank")
-                for t in range(4):
-                    nc.tensor.matmul(
-                        bank[:, t, :], lhsT=x_turned[b][:, 4 * g + t, :], rhs=w_sb[:], start=True, stop=True
-                    )
-                nc.scalar.copy(out=h_grouped[b][:, g, :, :], in_=bank[:].rearrange("p t f -> p f t"))
+        def multiply_x(b, g):
+            if g == 0:
+                h_grouped[b] = h_pool.tile([P, PASSES, F, 4], BF16, align_bytes=64, name="h_grouped")
+            bank = turn_psum.tile([P, 4, F], F32, tag="turn", name="h_bank")
+            for t in range(4):
+                nc.tensor.matmul(
+                    bank[:, t, :], lhsT=x_turned[b][:, 4 * g + t, :], rhs=w_sb[:], start=True, stop=True
+                )
+            nc.scalar.copy(out=h_grouped[b][:, g, :, :], in_=bank[:].rearrange("p t f -> p f t"))
 
         def quantise_h(b):
             cols = slice(b * PASSES * F, (b + 1) * PASSES * F)
@@ -235,72 +251,61 @@ def tile_spconvlayer_kernel(tc, x, adj, weight, bias, out):
                 in_=h_grouped[b][:].rearrange("p g f t -> p (g f t)"),
             )
 
-        load_adj(0, 0, 1)
-        load_adj(0, 1, 2)
+        for q in range(HALF):
+            load_adj(0, q, q + 1)
         load_x(0)
-        load_adj(0, 2, 3)
-        load_adj(0, 3, 4)
-        load_x(1)
-        load_adj(0, 4, 6)
-        load_adj(0, 6, 8)
         load_adj(1, 0, 2)
+        load_constants()
         load_adj(1, 2, 4)
-        load_x(2)
-        load_adj(1, 4, 6)
-        load_adj(1, 6, 8)
-        for b in range(3, B):
+        for half in range(2, ADJ_BUFS):
+            if half % 2 == 0 and half // 2 < B:
+                load_x(half // 2)
+            load_adj(half, 0, HALF)
+        for b in range(ADJ_BUFS // 2, B):
             load_x(b)
-        for b in range(2, 4):
-            load_adj(b, 0, 4)
-            load_adj(b, 4, 8)
 
-        half = NB // 2
-        for nb in range(half):
-            sum_rows(0, nb)
-        add_self_loops(0, 0, half)
-        invert_sums(0, 0, half)
+        for i in range(LEAD_SUM):
+            sum_rows(i)
+        invert_sums(0)
+        add_self_loops(0)
         transpose_x(0)
+        multiply_x(0, 0)
+        multiply_x(0, 1)
+        spread_bias()
 
         for step in range(ROWS + LAG_OUTPUT + 1):
+            half, q = divmod(step, HALF)
             b, k = divmod(step, NB)
-            following = b + 1
-            if following < B and k == 7:
-                invert_sums(following, 0, NB)
             if step < ROWS:
                 scale_rows(step)
-            if step < 2:
-                sum_rows(0, half + step)
-            if step == 2:
-                add_self_loops(0, half, NB)
-                invert_sums(0, half, NB)
-                nc.vector.tensor_copy(out=bias_f32[:], in_=bias_bf16[:])
-            if following < B:
-                if k < VECTOR_SUMS:
-                    sum_rows(following, k)
-                if k == 6:
-                    add_self_loops(following, 0, NB)
-            if k == 7 and b + 4 < B:
-                load_adj(b + 4, 0, half)
-                load_adj(b + 4, half, NB)
+            if 0 <= step - LAG_DIAGONAL < ROWS:
+                scale_diagonal(step - LAG_DIAGONAL)
+            if q == HALF - 1 and half + ADJ_BUFS < HALVES:
+                load_adj(half + ADJ_BUFS, 0, HALF)
             if 0 <= step - LAG_TRANSPOSE < ROWS:
                 transpose_rows(step - LAG_TRANSPOSE)
             if 0 <= step - LAG_COPY < ROWS:
                 copy_rows(step - LAG_COPY)
-            j, odd = divmod(step, 2)
-            if not odd and j < B:
-                multiply_x(j)
-            if odd and j + 1 < B:
-                transpose_x(j + 1)
-            if odd and 0 <= j - 1 < B:
-                quantise_h(j - 1)
-            if step == 0:
-                sum_rows(0, VECTOR_SUMS)
-                sum_rows(0, VECTOR_SUMS + 1)
-            if following < B and k in (2, 4):
-                sum_rows(following, VECTOR_SUMS + k // 2 - 1)
+            if step + LEAD_SUM < ROWS:
+                sum_rows(step + LEAD_SUM)
+            if half + 1 < HALVES and q == 2:
+                add_self_loops(half + 1)
+            if half + 1 < HALVES and q == 3:
+                invert_sums(half + 1)
+            if b + 1 < B:
+                if k == 0:
+                    transpose_x(b + 1)
+                if k == 2:
+                    multiply_x(b + 1, 0)
+                if k == 4:
+                    multiply_x(b + 1, 1)
+                if k == 6:
+                    quantise_h(b + 1)
+            if step == 1:
+                quantise_h(0)
+            if ends_group(step - LAG_OUTPUT):
+                output_group(group_of[step - LAG_OUTPUT])
             if ends_group(step - LAG_QUANTISE):
                 quantise_group(group_of[step - LAG_QUANTISE])
             if ends_group(step - LAG_MATMUL):
                 multiply_group(group_of[step - LAG_MATMUL])
-            if ends_group(step - LAG_OUTPUT):
-                output_group(group_of[step - LAG_OUTPUT])

@@ -23,6 +23,7 @@ FLOPS = 2 * B * N * N * F + 2 * B * N * F * F
 HALF = 4
 HALVES = ROWS // HALF
 ADJ_BUFS = 12
+SCALAR_SUMS = (1, 3, 5)
 GROUP_SIZES = [4] * (ROWS // 4 - 1) + [2, 1, 1]
 LEAD_SUM = 6
 LAG_DIAGONAL = 1
@@ -123,7 +124,7 @@ def tile_spconvlayer_kernel(tc, x, adj, weight, bias, out):
             if half not in sums:
                 sums[half] = norm_pool.tile([P, HALF], F32, name="sums")
             total = sums[half][:, q : q + 1]
-            if i % 2 == 0 and i != 4 or i == 3:
+            if i % NB not in SCALAR_SUMS and i != 4 or i == 3:
                 nc.vector.tensor_scalar(
                     out=unused_vector[:],
                     in0=row(i),

@@ -26,12 +26,12 @@ ADJ_BUFS = 12
 SCALAR_SUMS = (1, 3, 5)
 GROUP_SIZES = [4] * (ROWS // 4 - 1) + [2, 1, 1]
 LEAD_SUM = 6
-LAG_DIAGONAL = 1
-LAG_TRANSPOSE = 2
-LAG_COPY = 3
-LAG_QUANTISE = 6
-LAG_MATMUL = 7
-LAG_OUTPUT = 8
+LAG_DIAGONAL = 2
+LAG_TRANSPOSE = 3
+LAG_COPY = 4
+LAG_QUANTISE = 8
+LAG_MATMUL = 9
+LAG_OUTPUT = 10
 
 
 def tile_spconvlayer_kernel(tc, x, adj, weight, bias, out):
@@ -164,12 +164,11 @@ def tile_spconvlayer_kernel(tc, x, adj, weight, bias, out):
         def scale_diagonal(i):
             half, q = divmod(i, HALF)
             nb = i % NB
-            nc.vector.tensor_scalar(
+            nc.scalar.activation(
                 out=scaled[i][:, nb * P : (nb + 1) * P],
-                in0=with_loops[half][:, q, :],
-                scalar1=r[half][:, q : q + 1],
-                scalar2=None,
-                op0=ALU.mult,
+                in_=with_loops[half][:, q, :],
+                func=ACT.Copy,
+                scale=r[half][:, q : q + 1],
             )
 
         def transpose_rows(i):
@@ -279,6 +278,10 @@ def tile_spconvlayer_kernel(tc, x, adj, weight, bias, out):
             b, k = divmod(step, NB)
             if step < ROWS:
                 scale_rows(step)
+            if half + 1 < HALVES and q == 3:
+                invert_sums(half + 1)
+            if half + 1 < HALVES and q == 0:
+                add_self_loops(half + 1)
             if 0 <= step - LAG_DIAGONAL < ROWS:
                 scale_diagonal(step - LAG_DIAGONAL)
             if q == HALF - 1 and half + ADJ_BUFS < HALVES:
@@ -289,10 +292,6 @@ def tile_spconvlayer_kernel(tc, x, adj, weight, bias, out):
                 copy_rows(step - LAG_COPY)
             if step + LEAD_SUM < ROWS:
                 sum_rows(step + LEAD_SUM)
-            if half + 1 < HALVES and q == 2:
-                add_self_loops(half + 1)
-            if half + 1 < HALVES and q == 3:
-                invert_sums(half + 1)
             if b + 1 < B:
                 if k == 0:
                     transpose_x(b + 1)

@@ -23,9 +23,10 @@ FLOPS = 2 * B * N * N * F + 2 * B * N * F * F
 HALF = 4
 HALVES = ROWS // HALF
 ADJ_BUFS = 12
-SCALAR_SUMS = (1, 3, 5)
+SCALAR_SUMS = (1, 5)
 GROUP_SIZES = [4] * (ROWS // 4 - 1) + [2, 1, 1]
 LEAD_SUM = 6
+LEAD_LOOPS = 2
 LAG_DIAGONAL = 2
 LAG_TRANSPOSE = 3
 LAG_COPY = 4
@@ -40,6 +41,7 @@ def tile_spconvlayer_kernel(tc, x, adj, weight, bias, out):
         const = ctx.enter_context(tc.tile_pool(name="const", bufs=1))
         adj_pool = ctx.enter_context(tc.tile_pool(name="adj_pool", bufs=ADJ_BUFS))
         norm_pool = ctx.enter_context(tc.tile_pool(name="norm_pool", bufs=3))
+        loops_pool = ctx.enter_context(tc.tile_pool(name="loops_pool", bufs=6))
         scaled_pool = ctx.enter_context(tc.tile_pool(name="scaled_pool", bufs=6))
         group_pool = ctx.enter_context(tc.tile_pool(name="group_pool", bufs=3))
         h_pool = ctx.enter_context(tc.tile_pool(name="h_pool", bufs=2))
@@ -95,8 +97,8 @@ def tile_spconvlayer_kernel(tc, x, adj, weight, bias, out):
 
         def load_adj(half, lo, hi):
             if half not in adj_sb:
-                adj_sb[half] = adj_pool.tile([P, (HALF + 1) * N], BF16, name="adj_sb")
-            rows = adj_sb[half][:, 0 : HALF * N].rearrange("p (q c) -> p q c", c=N)
+                adj_sb[half] = adj_pool.tile([P, HALF * N], BF16, name="adj_sb")
+            rows = adj_sb[half][:].rearrange("p (q c) -> p q c", c=N)
             nc.sync.dma_start(out=rows[:, lo:hi, :], in_=adj_view[half][:, lo:hi, :])
 
         def load_x(b):
@@ -139,15 +141,11 @@ def tile_spconvlayer_kernel(tc, x, adj, weight, bias, out):
                     out=unused_scalar[:], in_=row(i), func=ACT.Copy, bias=1.0 / N, accum_out=total
                 )
 
-        def add_self_loops(half):
-            start = half % 2 * HALF * P
-            blocks = adj_sb[half][:, start : start + HALF * (N + P)].rearrange("p (q c) -> p q c", c=N + P)
-            with_loops[half] = norm_pool.tile([P, HALF, P], F32, name="with_loops")
-            nc.vector.tensor_tensor(
-                out=with_loops[half][:],
-                in0=blocks[:, :, 0:P],
-                in1=identity[:].unsqueeze(1).to_broadcast([P, HALF, P]),
-                op=ALU.add,
+        def add_self_loops(i):
+            nb = i % NB
+            with_loops[i] = loops_pool.tile([P, P], F32, name="with_loops")
+            nc.gpsimd.tensor_tensor(
+                out=with_loops[i][:], in0=row(i)[:, nb * P : (nb + 1) * P], in1=identity[:], op=ALU.add
             )
 
         def invert_sums(half):
@@ -166,7 +164,7 @@ def tile_spconvlayer_kernel(tc, x, adj, weight, bias, out):
             nb = i % NB
             nc.scalar.activation(
                 out=scaled[i][:, nb * P : (nb + 1) * P],
-                in_=with_loops[half][:, q, :],
+                in_=with_loops[i][:],
                 func=ACT.Copy,
                 scale=r[half][:, q : q + 1],
             )
@@ -267,7 +265,8 @@ def tile_spconvlayer_kernel(tc, x, adj, weight, bias, out):
         for i in range(LEAD_SUM):
             sum_rows(i)
         invert_sums(0)
-        add_self_loops(0)
+        for i in range(LEAD_LOOPS):
+            add_self_loops(i)
         transpose_x(0)
         multiply_x(0, 0)
         multiply_x(0, 1)
@@ -278,10 +277,10 @@ def tile_spconvlayer_kernel(tc, x, adj, weight, bias, out):
             b, k = divmod(step, NB)
             if step < ROWS:
                 scale_rows(step)
-            if half + 1 < HALVES and q == 3:
+            if half + 1 < HALVES and q == HALF - 1:
                 invert_sums(half + 1)
-            if half + 1 < HALVES and q == 0:
-                add_self_loops(half + 1)
+            if step + LEAD_LOOPS < ROWS:
+                add_self_loops(step + LEAD_LOOPS)
             if 0 <= step - LAG_DIAGONAL < ROWS:
                 scale_diagonal(step - LAG_DIAGONAL)
             if q == HALF - 1 and half + ADJ_BUFS < HALVES:

@@ -23,16 +23,16 @@ FLOPS = 2 * B * N * N * F + 2 * B * N * F * F
 HALF = 4
 HALVES = ROWS // HALF
 ADJ_BUFS = 12
-SCALAR_SUMS = (1, 5)
+SCALAR_SUMS = (1, 5, 7)
 GROUP_SIZES = [4] * (ROWS // 4 - 1) + [2, 1, 1]
-LEAD_SUM = 6
-LEAD_LOOPS = 2
-LAG_DIAGONAL = 2
-LAG_TRANSPOSE = 3
+LEAD_VECTOR_SUM = 6
+LEAD_SCALAR_SUM = 10
+LEAD_LOOPS = 1
+LAG_TRANSPOSE = 2
 LAG_COPY = 4
 LAG_QUANTISE = 8
-LAG_MATMUL = 9
-LAG_OUTPUT = 10
+LAG_MATMUL = 10
+LAG_OUTPUT = 12
 
 
 def tile_spconvlayer_kernel(tc, x, adj, weight, bias, out):
@@ -44,6 +44,7 @@ def tile_spconvlayer_kernel(tc, x, adj, weight, bias, out):
         loops_pool = ctx.enter_context(tc.tile_pool(name="loops_pool", bufs=6))
         scaled_pool = ctx.enter_context(tc.tile_pool(name="scaled_pool", bufs=6))
         group_pool = ctx.enter_context(tc.tile_pool(name="group_pool", bufs=3))
+        result_pool = ctx.enter_context(tc.tile_pool(name="result_pool", bufs=5))
         h_pool = ctx.enter_context(tc.tile_pool(name="h_pool", bufs=2))
         turn_psum = ctx.enter_context(tc.psum_pool(name="turn_psum", bufs=6))
         product_psum = ctx.enter_context(tc.psum_pool(name="product_psum", bufs=2))
@@ -121,12 +122,15 @@ def tile_spconvlayer_kernel(tc, x, adj, weight, bias, out):
             half, q = divmod(i, HALF)
             return adj_sb[half][:, q * N : (q + 1) * N]
 
+        def scalar_sums(i):
+            return i % NB in SCALAR_SUMS
+
         def sum_rows(i):
             half, q = divmod(i, HALF)
             if half not in sums:
                 sums[half] = norm_pool.tile([P, HALF], F32, name="sums")
             total = sums[half][:, q : q + 1]
-            if i % NB not in SCALAR_SUMS and i != 4 or i == 3:
+            if not scalar_sums(i):
                 nc.vector.tensor_scalar(
                     out=unused_vector[:],
                     in0=row(i),
@@ -162,11 +166,13 @@ def tile_spconvlayer_kernel(tc, x, adj, weight, bias, out):
         def scale_diagonal(i):
             half, q = divmod(i, HALF)
             nb = i % NB
-            nc.scalar.activation(
+            nc.gpsimd.tensor_scalar(
                 out=scaled[i][:, nb * P : (nb + 1) * P],
-                in_=with_loops[i][:],
-                func=ACT.Copy,
-                scale=r[half][:, q : q + 1],
+                in0=with_loops[i][:],
+                scalar1=r[half][:, q : q + 1],
+                scalar2=0.0,
+                op0=ALU.mult,
+                op1=ALU.add,
             )
 
         def transpose_rows(i):
@@ -213,7 +219,7 @@ def tile_spconvlayer_kernel(tc, x, adj, weight, bias, out):
         def output_group(u):
             b, nb = divmod(first_row[u], NB)
             size = GROUP_SIZES[u]
-            result = group_pool.tile([P, size, F], F32, name="result")
+            result = result_pool.tile([P, size, F], F32, name="result")
             nc.vector.scalar_tensor_tensor(
                 out=result[:],
                 in0=product[u][:],
@@ -262,35 +268,50 @@ def tile_spconvlayer_kernel(tc, x, adj, weight, bias, out):
         for b in range(ADJ_BUFS // 2, B):
             load_x(b)
 
-        for i in range(LEAD_SUM):
+        first_sums = [i for i in range(LEAD_SCALAR_SUM) if scalar_sums(i)]
+        for i in range(HALF):
+            if not scalar_sums(i):
+                sum_rows(i)
+        for i in first_sums[:2]:
             sum_rows(i)
         invert_sums(0)
         for i in range(LEAD_LOOPS):
             add_self_loops(i)
         transpose_x(0)
+        sum_rows(first_sums[2])
         multiply_x(0, 0)
         multiply_x(0, 1)
+        for i in first_sums[3:]:
+            sum_rows(i)
         spread_bias()
 
         for step in range(ROWS + LAG_OUTPUT + 1):
             half, q = divmod(step, HALF)
             b, k = divmod(step, NB)
+            if ends_group(step - LAG_MATMUL):
+                multiply_group(group_of[step - LAG_MATMUL])
+            if ends_group(step - LAG_QUANTISE):
+                quantise_group(group_of[step - LAG_QUANTISE])
             if step < ROWS:
                 scale_rows(step)
-            if half + 1 < HALVES and q == HALF - 1:
-                invert_sums(half + 1)
+                scale_diagonal(step)
             if step + LEAD_LOOPS < ROWS:
                 add_self_loops(step + LEAD_LOOPS)
-            if 0 <= step - LAG_DIAGONAL < ROWS:
-                scale_diagonal(step - LAG_DIAGONAL)
             if q == HALF - 1 and half + ADJ_BUFS < HALVES:
                 load_adj(half + ADJ_BUFS, 0, HALF)
             if 0 <= step - LAG_TRANSPOSE < ROWS:
                 transpose_rows(step - LAG_TRANSPOSE)
             if 0 <= step - LAG_COPY < ROWS:
                 copy_rows(step - LAG_COPY)
-            if step + LEAD_SUM < ROWS:
-                sum_rows(step + LEAD_SUM)
+            for i in range(HALF if step == 0 else step + LEAD_VECTOR_SUM, min(step + LEAD_VECTOR_SUM + 1, ROWS)):
+                if not scalar_sums(i):
+                    sum_rows(i)
+            if step + LEAD_SCALAR_SUM < ROWS and scalar_sums(step + LEAD_SCALAR_SUM):
+                sum_rows(step + LEAD_SCALAR_SUM)
+            if ends_group(step - LAG_OUTPUT):
+                output_group(group_of[step - LAG_OUTPUT])
+            if half + 1 < HALVES and q == 2:
+                invert_sums(half + 1)
             if b + 1 < B:
                 if k == 0:
                     transpose_x(b + 1)
@@ -298,13 +319,7 @@ def tile_spconvlayer_kernel(tc, x, adj, weight, bias, out):
                     multiply_x(b + 1, 0)
                 if k == 4:
                     multiply_x(b + 1, 1)
-                if k == 6:
-                    quantise_h(b + 1)
-            if step == 1:
+            if step == 5:
                 quantise_h(0)
-            if ends_group(step - LAG_OUTPUT):
-                output_group(group_of[step - LAG_OUTPUT])
-            if ends_group(step - LAG_QUANTISE):
-                quantise_group(group_of[step - LAG_QUANTISE])
-            if ends_group(step - LAG_MATMUL):
-                multiply_group(group_of[step - LAG_MATMUL])
+            if 0 < b < B and k == 1:
+                quantise_h(b)

@@ -23,16 +23,20 @@ FLOPS = 2 * B * N * N * F + 2 * B * N * F * F
 HALF = 4
 HALVES = ROWS // HALF
 ADJ_BUFS = 12
-SCALAR_SUMS = (1, 5, 7)
+SCALAR_SUMS = (1, 5, 7, 9, 13)
+TENSOR_SUMS = SCALAR_SUMS[:4]
 GROUP_SIZES = [4] * (ROWS // 4 - 1) + [2, 1, 1]
+LAST = 6
 LEAD_VECTOR_SUM = 6
 LEAD_SCALAR_SUM = 10
-LEAD_LOOPS = 1
-LAG_TRANSPOSE = 2
-LAG_COPY = 4
-LAG_QUANTISE = 8
-LAG_MATMUL = 10
-LAG_OUTPUT = 12
+LEAD_LOOPS = 2
+LAG_DIAGONAL = 2
+LAG_VECTOR_DIAGONAL = 1
+LAG_TRANSPOSE = 3
+LAG_COPY = 5
+LAG_QUANTISE = 12
+LAG_MATMUL = 14
+LAG_OUTPUT = 16
 
 
 def tile_spconvlayer_kernel(tc, x, adj, weight, bias, out):
@@ -43,7 +47,7 @@ def tile_spconvlayer_kernel(tc, x, adj, weight, bias, out):
         norm_pool = ctx.enter_context(tc.tile_pool(name="norm_pool", bufs=3))
         loops_pool = ctx.enter_context(tc.tile_pool(name="loops_pool", bufs=6))
         scaled_pool = ctx.enter_context(tc.tile_pool(name="scaled_pool", bufs=6))
-        group_pool = ctx.enter_context(tc.tile_pool(name="group_pool", bufs=3))
+        group_pool = ctx.enter_context(tc.tile_pool(name="group_pool", bufs=4))
         result_pool = ctx.enter_context(tc.tile_pool(name="result_pool", bufs=5))
         h_pool = ctx.enter_context(tc.tile_pool(name="h_pool", bufs=2))
         turn_psum = ctx.enter_context(tc.psum_pool(name="turn_psum", bufs=6))
@@ -123,7 +127,7 @@ def tile_spconvlayer_kernel(tc, x, adj, weight, bias, out):
             return adj_sb[half][:, q * N : (q + 1) * N]
 
         def scalar_sums(i):
-            return i % NB in SCALAR_SUMS
+            return i % (2 * NB) in SCALAR_SUMS
 
         def sum_rows(i):
             half, q = divmod(i, HALF)
@@ -139,6 +143,19 @@ def tile_spconvlayer_kernel(tc, x, adj, weight, bias, out):
                     op0=ALU.mult,
                     op1=ALU.add,
                     accum_out=total,
+                )
+            elif i in TENSOR_SUMS:
+                bank = turn_psum.tile([P, P], F32, tag="turn", name="sum_bank")
+                for j in range(NB):
+                    nc.tensor.matmul(
+                        bank[:],
+                        lhsT=identity[:],
+                        rhs=row(i)[:, j * P : (j + 1) * P],
+                        start=(j == 0),
+                        stop=(j == NB - 1),
+                    )
+                nc.scalar.activation(
+                    out=unused_scalar[:, 0:P], in_=bank[:], func=ACT.Copy, bias=1.0 / P, accum_out=total
                 )
             else:
                 nc.scalar.activation(
@@ -166,14 +183,12 @@ def tile_spconvlayer_kernel(tc, x, adj, weight, bias, out):
         def scale_diagonal(i):
             half, q = divmod(i, HALF)
             nb = i % NB
-            nc.gpsimd.tensor_scalar(
-                out=scaled[i][:, nb * P : (nb + 1) * P],
-                in0=with_loops[i][:],
-                scalar1=r[half][:, q : q + 1],
-                scalar2=0.0,
-                op0=ALU.mult,
-                op1=ALU.add,
-            )
+            block = scaled[i][:, nb * P : (nb + 1) * P]
+            factor = r[half][:, q : q + 1]
+            if i < ROWS - LAST:
+                nc.scalar.activation(out=block, in_=with_loops[i][:], func=ACT.Copy, scale=factor)
+            else:
+                nc.vector.tensor_scalar(out=block, in0=with_loops[i][:], scalar1=factor, scalar2=None, op0=ALU.mult)
 
         def transpose_rows(i):
             turned[i] = turn_psum.tile([P, PASSES, 2, P], F32, tag="turn", name="turned")
@@ -188,7 +203,8 @@ def tile_spconvlayer_kernel(tc, x, adj, weight, bias, out):
             q = i - first_row[u]
             if q == 0:
                 grouped[u] = group_pool.tile([P, GROUP_SIZES[u] * N], BF16, align_bytes=64, name="grouped")
-            nc.scalar.copy(
+            copy = nc.vector.tensor_copy if i >= ROWS - LAST and i % 2 == 1 else nc.scalar.copy
+            copy(
                 out=grouped[u][:, q * N : (q + 1) * N].bitcast(F32).rearrange("p (g n e) -> p g n e", g=PASSES, e=2),
                 in_=turned[i][:].rearrange("p g e n -> p g n e"),
             )
@@ -262,9 +278,9 @@ def tile_spconvlayer_kernel(tc, x, adj, weight, bias, out):
         load_constants()
         load_adj(1, 2, 4)
         for half in range(2, ADJ_BUFS):
+            load_adj(half, 0, HALF)
             if half % 2 == 0 and half // 2 < B:
                 load_x(half // 2)
-            load_adj(half, 0, HALF)
         for b in range(ADJ_BUFS // 2, B):
             load_x(b)
 
@@ -294,7 +310,10 @@ def tile_spconvlayer_kernel(tc, x, adj, weight, bias, out):
                 quantise_group(group_of[step - LAG_QUANTISE])
             if step < ROWS:
                 scale_rows(step)
-                scale_diagonal(step)
+            if 0 <= step - LAG_DIAGONAL < ROWS - LAST:
+                scale_diagonal(step - LAG_DIAGONAL)
+            if ROWS - LAST <= step - LAG_VECTOR_DIAGONAL < ROWS:
+                scale_diagonal(step - LAG_VECTOR_DIAGONAL)
             if step + LEAD_LOOPS < ROWS:
                 add_self_loops(step + LEAD_LOOPS)
             if q == HALF - 1 and half + ADJ_BUFS < HALVES:
@@ -313,13 +332,13 @@ def tile_spconvlayer_kernel(tc, x, adj, weight, bias, out):
             if half + 1 < HALVES and q == 2:
                 invert_sums(half + 1)
             if b + 1 < B:
-                if k == 0:
-                    transpose_x(b + 1)
                 if k == 2:
-                    multiply_x(b + 1, 0)
+                    transpose_x(b + 1)
                 if k == 4:
+                    multiply_x(b + 1, 0)
+                if k == 6:
                     multiply_x(b + 1, 1)
             if step == 5:
                 quantise_h(0)
-            if 0 < b < B and k == 1:
+            if 0 < b < B and k == 3:
                 quantise_h(b)

@@ -20,43 +20,41 @@ ROWS = B * NB
 PASSES = N // (4 * P)
 FLOPS = 2 * B * N * N * F + 2 * B * N * F * F
 
-HALF = 4
-HALVES = ROWS // HALF
-ADJ_BUFS = 12
-SCALAR_SUMS = (1, 5, 7, 9, 13)
-TENSOR_SUMS = SCALAR_SUMS[:4]
-GROUP_SIZES = [4] * (ROWS // 4 - 1) + [2, 1, 1]
-LAST = 6
-LEAD_VECTOR_SUM = 6
+QUAD = 4
+RUN = P // QUAD
+CHUNK = 4
+CHUNKS = ROWS // CHUNK
+ADJ_BUFS = 8
+SCALAR_SUMS = [1, 5, 7, 9, 11] + [i for i in range(24, ROWS) if i % 2 == 1]
+TENSOR_SUMS = (5, 7, 9, 11)
+LEAD_VECTOR_SUM = 8
 LEAD_SCALAR_SUM = 10
-LEAD_LOOPS = 2
-LAG_DIAGONAL = 2
-LAG_VECTOR_DIAGONAL = 1
-LAG_TRANSPOSE = 3
-LAG_COPY = 5
-LAG_QUANTISE = 12
-LAG_MATMUL = 14
-LAG_OUTPUT = 16
-
+LAG_TRANSPOSE = 5
+LAG_COPY = 7
+H_READY = 24
+QUANTISE_AT = [CHUNK * c + 13 for c in range(CHUNKS)]
+MULTIPLY_AT = [max(CHUNK * c + 14, H_READY + 2 * c) for c in range(CHUNKS)]
+OUTPUT_AT = [step + 4 for step in MULTIPLY_AT]
+STEPS = OUTPUT_AT[-1] + 1
 
 def tile_spconvlayer_kernel(tc, x, adj, weight, bias, out):
     nc = tc.nc
     with ExitStack() as ctx:
         const = ctx.enter_context(tc.tile_pool(name="const", bufs=1))
         adj_pool = ctx.enter_context(tc.tile_pool(name="adj_pool", bufs=ADJ_BUFS))
-        norm_pool = ctx.enter_context(tc.tile_pool(name="norm_pool", bufs=3))
-        loops_pool = ctx.enter_context(tc.tile_pool(name="loops_pool", bufs=6))
-        scaled_pool = ctx.enter_context(tc.tile_pool(name="scaled_pool", bufs=6))
-        group_pool = ctx.enter_context(tc.tile_pool(name="group_pool", bufs=4))
-        result_pool = ctx.enter_context(tc.tile_pool(name="result_pool", bufs=5))
+        norm_pool = ctx.enter_context(tc.tile_pool(name="norm_pool", bufs=6))
+        scaled_pool = ctx.enter_context(tc.tile_pool(name="scaled_pool", bufs=3))
+        words_pool = ctx.enter_context(tc.tile_pool(name="words_pool", bufs=4))
+        codes_pool = ctx.enter_context(tc.tile_pool(name="codes_pool", bufs=6))
+        result_pool = ctx.enter_context(tc.tile_pool(name="result_pool", bufs=4))
         h_pool = ctx.enter_context(tc.tile_pool(name="h_pool", bufs=2))
         turn_psum = ctx.enter_context(tc.psum_pool(name="turn_psum", bufs=6))
         product_psum = ctx.enter_context(tc.psum_pool(name="product_psum", bufs=2))
         ctx.enter_context(tc.manual_schedule())
 
         x_view = x.rearrange("b (g p t) m a -> b p g (t m a)", p=P, t=4)
-        adj_view = adj.rearrange("b (half q p) c -> (b half) p q c", p=P, q=HALF)
-        out_view = out.rearrange("b (nb p) u w -> b p nb (u w)", p=P)
+        adj_view = adj.rearrange("b (s q n) c -> b s n q c", q=CHUNK, n=RUN)
+        out_view = out.rearrange("(d b) (s p) u w -> d s p b (u w)", b=QUAD, p=P)
 
         warm = const.tile([P, 2], F32)
         nc.vector.memset(warm[:], 0.0)
@@ -66,6 +64,18 @@ def tile_spconvlayer_kernel(tc, x, adj, weight, bias, out):
         make_identity(nc, identity[:])
         identity_f32 = const.tile([P, P], F32)
         make_identity(nc, identity_f32[:])
+        permutation = const.tile([P, P], F32)
+        nc.vector.tensor_copy(
+            out=permutation[:].rearrange("p (b n) -> p b n", b=QUAD),
+            in_=identity_f32[:].rearrange("p (n b) -> p b n", b=QUAD),
+        )
+        loops = const.tile([P, RUN], F32)
+        nc.vector.tensor_reduce(
+            out=loops[:],
+            in_=identity[:].rearrange("p (n b) -> p n b", b=QUAD),
+            axis=mybir.AxisListType.X,
+            op=ALU.add,
+        )
         ones = const.tile([P, P], BF16)
         nc.gpsimd.memset(ones[:], 1.0)
         bias_row = const.tile([P, F], BF16)
@@ -82,29 +92,24 @@ def tile_spconvlayer_kernel(tc, x, adj, weight, bias, out):
         sums = {}
         r = {}
         with_loops = {}
-        x_turned = {}
-        h_grouped = {}
         scaled = {}
-        turned = {}
         grouped = {}
         codes = {}
         scales = {}
         product = {}
+        x_turned = {}
+        h_grouped = {}
+        turned = {}
 
-        first_row = [sum(GROUP_SIZES[:u]) for u in range(len(GROUP_SIZES))]
-        group_of = {}
-        for u in range(len(GROUP_SIZES)):
-            for q in range(GROUP_SIZES[u]):
-                group_of[first_row[u] + q] = u
-
-        def ends_group(i):
-            return 0 <= i < ROWS and group_of.get(i + 1, -1) != group_of[i]
-
-        def load_adj(half, lo, hi):
-            if half not in adj_sb:
-                adj_sb[half] = adj_pool.tile([P, HALF * N], BF16, name="adj_sb")
-            rows = adj_sb[half][:].rearrange("p (q c) -> p q c", c=N)
-            nc.sync.dma_start(out=rows[:, lo:hi, :], in_=adj_view[half][:, lo:hi, :])
+        def load_adj(chunk, lo, hi):
+            if chunk not in adj_sb:
+                adj_sb[chunk] = adj_pool.tile([P, (CHUNK + 1) * N], BF16, name="adj_sb")
+            rows = adj_sb[chunk][:, 0 : CHUNK * N].rearrange("p (q c) -> p q c", c=N)
+            d, part = divmod(chunk, CHUNKS * QUAD // B)
+            for b in range(QUAD):
+                nc.sync.dma_start(
+                    out=rows[b:P:QUAD, lo:hi, :], in_=adj_view[QUAD * d + b][part][:, lo:hi, :]
+                )
 
         def load_x(b):
             nc.sync.dma_start(out=x_sb[:, b, :, :], in_=x_view[b])
@@ -123,18 +128,26 @@ def tile_spconvlayer_kernel(tc, x, adj, weight, bias, out):
             nc.scalar.copy(out=bias_f32[:], in_=bank[:])
 
         def row(i):
-            half, q = divmod(i, HALF)
-            return adj_sb[half][:, q * N : (q + 1) * N]
+            chunk, q = divmod(i, CHUNK)
+            return adj_sb[chunk][:, q * N : (q + 1) * N]
 
-        def scalar_sums(i):
-            return i % (2 * NB) in SCALAR_SUMS
+        def on_diagonal(tile, chunk):
+            start = chunk * P % N
+            wide = tile[:, start : start + CHUNK * (N + RUN)]
+            return wide.rearrange("p (q c) -> p q c", c=N + RUN)[:, :, 0:RUN]
+
+        def vector_lead(step):
+            return min(LEAD_VECTOR_SUM, CHUNK + step // 2) if step >= 0 else CHUNK
+
+        def scalar_lead(step):
+            return min(LEAD_SCALAR_SUM, 2 * CHUNK + 2 * step)
 
         def sum_rows(i):
-            half, q = divmod(i, HALF)
-            if half not in sums:
-                sums[half] = norm_pool.tile([P, HALF], F32, name="sums")
-            total = sums[half][:, q : q + 1]
-            if not scalar_sums(i):
+            chunk, q = divmod(i, CHUNK)
+            if chunk not in sums:
+                sums[chunk] = norm_pool.tile([P, CHUNK], F32, name="sums")
+            total = sums[chunk][:, q : q + 1]
+            if i not in SCALAR_SUMS:
                 nc.vector.tensor_scalar(
                     out=unused_vector[:],
                     in0=row(i),
@@ -162,89 +175,96 @@ def tile_spconvlayer_kernel(tc, x, adj, weight, bias, out):
                     out=unused_scalar[:], in_=row(i), func=ACT.Copy, bias=1.0 / N, accum_out=total
                 )
 
-        def add_self_loops(i):
-            nb = i % NB
-            with_loops[i] = loops_pool.tile([P, P], F32, name="with_loops")
-            nc.gpsimd.tensor_tensor(
-                out=with_loops[i][:], in0=row(i)[:, nb * P : (nb + 1) * P], in1=identity[:], op=ALU.add
+        def add_self_loops(chunk):
+            with_loops[chunk] = norm_pool.tile([P, CHUNK, RUN], F32, name="with_loops")
+            nc.vector.tensor_tensor(
+                out=with_loops[chunk][:],
+                in0=on_diagonal(adj_sb[chunk], chunk),
+                in1=loops[:].unsqueeze(1).to_broadcast([P, CHUNK, RUN]),
+                op=ALU.add,
             )
 
-        def invert_sums(half):
-            r[half] = norm_pool.tile([P, HALF], F32, name="r")
-            nc.vector.reciprocal(r[half][:], sums[half][:])
+        def invert_sums(chunk):
+            r[chunk] = norm_pool.tile([P, CHUNK], F32, name="r")
+            nc.vector.reciprocal(r[chunk][:], sums[chunk][:])
 
         def scale_rows(i):
-            half, q = divmod(i, HALF)
-            scaled[i] = scaled_pool.tile([P, N], BF16, name="scaled")
+            chunk, q = divmod(i, CHUNK)
+            if q == 0:
+                scaled[chunk] = scaled_pool.tile([P, (CHUNK + 1) * N], BF16, name="scaled")
             nc.vector.tensor_scalar(
-                out=scaled[i][:], in0=row(i), scalar1=r[half][:, q : q + 1], scalar2=None, op0=ALU.mult
+                out=scaled[chunk][:, q * N : (q + 1) * N],
+                in0=row(i),
+                scalar1=r[chunk][:, q : q + 1],
+                scalar2=None,
+                op0=ALU.mult,
             )
 
-        def scale_diagonal(i):
-            half, q = divmod(i, HALF)
-            nb = i % NB
-            block = scaled[i][:, nb * P : (nb + 1) * P]
-            factor = r[half][:, q : q + 1]
-            if i < ROWS - LAST:
-                nc.scalar.activation(out=block, in_=with_loops[i][:], func=ACT.Copy, scale=factor)
-            else:
-                nc.vector.tensor_scalar(out=block, in0=with_loops[i][:], scalar1=factor, scalar2=None, op0=ALU.mult)
+        def scale_diagonal(chunk):
+            nc.vector.tensor_tensor(
+                out=on_diagonal(scaled[chunk], chunk),
+                in0=with_loops[chunk][:],
+                in1=r[chunk][:].unsqueeze(2).to_broadcast([P, CHUNK, RUN]),
+                op=ALU.mult,
+            )
 
         def transpose_rows(i):
-            turned[i] = turn_psum.tile([P, PASSES, 2, P], F32, tag="turn", name="turned")
-            pairs = scaled[i][:].bitcast(F32)
+            chunk, q = divmod(i, CHUNK)
+            turned[i] = turn_psum.tile([P, 2, PASSES, P], F32, tag="turn", name="turned")
+            pairs = scaled[chunk][:, q * N : (q + 1) * N].bitcast(F32)
             for g in range(PASSES):
                 for e in range(2):
                     source = pairs[:, 2 * P * g + e : 2 * P * (g + 1) : 2]
-                    nc.tensor.transpose(turned[i][:, g, e, :], source, identity_f32[:])
+                    nc.tensor.transpose(turned[i][:, e, g, :], source, permutation[:])
 
         def copy_rows(i):
-            u = group_of[i]
-            q = i - first_row[u]
+            chunk, q = divmod(i, CHUNK)
             if q == 0:
-                grouped[u] = group_pool.tile([P, GROUP_SIZES[u] * N], BF16, align_bytes=64, name="grouped")
-            copy = nc.vector.tensor_copy if i >= ROWS - LAST and i % 2 == 1 else nc.scalar.copy
-            copy(
-                out=grouped[u][:, q * N : (q + 1) * N].bitcast(F32).rearrange("p (g n e) -> p g n e", g=PASSES, e=2),
-                in_=turned[i][:].rearrange("p g e n -> p g n e"),
+                grouped[chunk] = words_pool.tile([P, CHUNK * N], BF16, align_bytes=64, name="grouped")
+            words = grouped[chunk][:].bitcast(F32).rearrange("p (k n e) -> p k n e", n=P, e=2)
+            nc.scalar.copy(
+                out=words[:, :, q * RUN : (q + 1) * RUN, :],
+                in_=turned[i][:].rearrange("p e g (b n) -> p (g b) n e", b=QUAD),
             )
 
-        def quantise_group(u):
-            width = GROUP_SIZES[u] * PASSES * P
-            codes[u] = group_pool.tile([P, width], U32, align_bytes=64, name="codes")
-            scales[u] = group_pool.tile([P, width], U8, align_bytes=64, name="scales")
-            nc.vector.quantize_mx(out=codes[u][:].bitcast(FP8X4), scales=scales[u][:], in_=grouped[u][:])
+        def quantise_chunk(chunk):
+            width = QUAD * PASSES * P
+            codes[chunk] = codes_pool.tile([P, width], U32, align_bytes=64, name="codes")
+            scales[chunk] = codes_pool.tile([P, width], U8, align_bytes=64, name="scales")
+            nc.vector.quantize_mx(
+                out=codes[chunk][:].bitcast(FP8X4), scales=scales[chunk][:], in_=grouped[chunk][:]
+            )
 
-        def multiply_group(u):
-            b = first_row[u] // NB
-            product[u] = product_psum.tile([P, GROUP_SIZES[u], F], F32, name="product")
-            for q in range(GROUP_SIZES[u]):
+        def multiply_chunk(chunk):
+            d = chunk // (CHUNKS * QUAD // B)
+            product[chunk] = product_psum.tile([P, QUAD, F], F32, name="product")
+            for b in range(QUAD):
                 for g in range(PASSES):
-                    a_cols = slice((q * PASSES + g) * P, (q * PASSES + g + 1) * P)
-                    h_cols = slice((b * PASSES + g) * F, (b * PASSES + g + 1) * F)
+                    a_cols = slice((g * QUAD + b) * P, (g * QUAD + b + 1) * P)
+                    h_first = ((QUAD * d + b) * PASSES + g) * F
+                    h_cols = slice(h_first, h_first + F)
                     nc.tensor.matmul_mx(
-                        out=product[u][:, q, :],
-                        lhsT=codes[u][:, a_cols].bitcast(FP8X4),
-                        lhsT_scale=scales[u][:, a_cols],
+                        out=product[chunk][:, b, :],
+                        lhsT=codes[chunk][:, a_cols].bitcast(FP8X4),
+                        lhsT_scale=scales[chunk][:, a_cols],
                         rhs=h_codes[:, h_cols].bitcast(FP8X4),
                         rhs_scale=h_scales[:, h_cols],
                         start=(g == 0),
                         stop=(g == PASSES - 1),
                     )
 
-        def output_group(u):
-            b, nb = divmod(first_row[u], NB)
-            size = GROUP_SIZES[u]
-            result = result_pool.tile([P, size, F], F32, name="result")
+        def output_chunk(chunk):
+            d, part = divmod(chunk, CHUNKS * QUAD // B)
+            result = result_pool.tile([P, QUAD, F], F32, name="result")
             nc.vector.scalar_tensor_tensor(
                 out=result[:],
-                in0=product[u][:],
+                in0=product[chunk][:],
                 scalar=0.0,
-                in1=bias_f32[:].unsqueeze(1).to_broadcast([P, size, F]),
+                in1=bias_f32[:].unsqueeze(1).to_broadcast([P, QUAD, F]),
                 op0=ALU.max,
                 op1=ALU.add,
             )
-            nc.sync.dma_start(out=out_view[b][:, nb : nb + size, :], in_=result[:])
+            nc.sync.dma_start(out=out_view[d][part], in_=result[:])
 
         def transpose_x(b):
             bank = turn_psum.tile([P, NB, P], BF16, tag="turn", name="x_bank")
@@ -271,74 +291,71 @@ def tile_spconvlayer_kernel(tc, x, adj, weight, bias, out):
                 in_=h_grouped[b][:].rearrange("p g f t -> p (g f t)"),
             )
 
-        for q in range(HALF):
-            load_adj(0, q, q + 1)
-        load_x(0)
-        load_adj(1, 0, 2)
+        load_adj(0, 0, 2)
+        load_adj(0, 2, 4)
+        load_adj(1, 0, 4)
         load_constants()
-        load_adj(1, 2, 4)
-        for half in range(2, ADJ_BUFS):
-            load_adj(half, 0, HALF)
-            if half % 2 == 0 and half // 2 < B:
-                load_x(half // 2)
-        for b in range(ADJ_BUFS // 2, B):
+        load_x(0)
+        load_x(1)
+        load_adj(2, 0, 4)
+        load_x(2)
+        load_adj(3, 0, 4)
+        load_x(3)
+        for chunk in range(4, ADJ_BUFS):
+            load_adj(chunk, 0, CHUNK)
+        for b in range(4, B):
             load_x(b)
 
-        first_sums = [i for i in range(LEAD_SCALAR_SUM) if scalar_sums(i)]
-        for i in range(HALF):
-            if not scalar_sums(i):
-                sum_rows(i)
-        for i in first_sums[:2]:
+        for i in range(CHUNK):
             sum_rows(i)
         invert_sums(0)
-        for i in range(LEAD_LOOPS):
-            add_self_loops(i)
-        transpose_x(0)
-        sum_rows(first_sums[2])
-        multiply_x(0, 0)
-        multiply_x(0, 1)
-        for i in first_sums[3:]:
-            sum_rows(i)
-        spread_bias()
+        add_self_loops(0)
+        for i in range(CHUNK, 2 * CHUNK):
+            if i in SCALAR_SUMS:
+                sum_rows(i)
 
-        for step in range(ROWS + LAG_OUTPUT + 1):
-            half, q = divmod(step, HALF)
-            b, k = divmod(step, NB)
-            if ends_group(step - LAG_MATMUL):
-                multiply_group(group_of[step - LAG_MATMUL])
-            if ends_group(step - LAG_QUANTISE):
-                quantise_group(group_of[step - LAG_QUANTISE])
+        h_start = [3 * b if b < QUAD else 14 + 6 * (b - QUAD) for b in range(B)]
+
+        for step in range(STEPS):
+            chunk, q = divmod(step, CHUNK)
+            for c in range(CHUNKS):
+                if step == OUTPUT_AT[c]:
+                    output_chunk(c)
+            for c in range(CHUNKS):
+                if step == MULTIPLY_AT[c]:
+                    multiply_chunk(c)
             if step < ROWS:
                 scale_rows(step)
-            if 0 <= step - LAG_DIAGONAL < ROWS - LAST:
-                scale_diagonal(step - LAG_DIAGONAL)
-            if ROWS - LAST <= step - LAG_VECTOR_DIAGONAL < ROWS:
-                scale_diagonal(step - LAG_VECTOR_DIAGONAL)
-            if step + LEAD_LOOPS < ROWS:
-                add_self_loops(step + LEAD_LOOPS)
-            if q == HALF - 1 and half + ADJ_BUFS < HALVES:
-                load_adj(half + ADJ_BUFS, 0, HALF)
+            if q == 0 and 1 <= chunk <= CHUNKS:
+                scale_diagonal(chunk - 1)
+            if q == CHUNK - 1 and chunk + ADJ_BUFS < CHUNKS:
+                load_adj(chunk + ADJ_BUFS, 0, CHUNK)
             if 0 <= step - LAG_TRANSPOSE < ROWS:
                 transpose_rows(step - LAG_TRANSPOSE)
             if 0 <= step - LAG_COPY < ROWS:
                 copy_rows(step - LAG_COPY)
-            for i in range(HALF if step == 0 else step + LEAD_VECTOR_SUM, min(step + LEAD_VECTOR_SUM + 1, ROWS)):
-                if not scalar_sums(i):
+            for c in range(CHUNKS):
+                if step == QUANTISE_AT[c]:
+                    quantise_chunk(c)
+            if step == 1:
+                spread_bias()
+            for b in range(B):
+                if step == h_start[b]:
+                    transpose_x(b)
+                if step == h_start[b] + 1:
+                    multiply_x(b, 0)
+                if step == h_start[b] + 2:
+                    multiply_x(b, 1)
+            for i in range(vector_lead(step - 1) + step, min(vector_lead(step) + step + 1, ROWS)):
+                if i not in SCALAR_SUMS:
                     sum_rows(i)
-            if step + LEAD_SCALAR_SUM < ROWS and scalar_sums(step + LEAD_SCALAR_SUM):
-                sum_rows(step + LEAD_SCALAR_SUM)
-            if ends_group(step - LAG_OUTPUT):
-                output_group(group_of[step - LAG_OUTPUT])
-            if half + 1 < HALVES and q == 2:
-                invert_sums(half + 1)
-            if b + 1 < B:
-                if k == 2:
-                    transpose_x(b + 1)
-                if k == 4:
-                    multiply_x(b + 1, 0)
-                if k == 6:
-                    multiply_x(b + 1, 1)
-            if step == 5:
-                quantise_h(0)
-            if 0 < b < B and k == 3:
-                quantise_h(b)
+            for i in range(2 * CHUNK if step == 0 else step + scalar_lead(step - 1), step + scalar_lead(step) + 1):
+                if i in SCALAR_SUMS:
+                    sum_rows(i)
+            if q == 1 and chunk + 1 < CHUNKS:
+                add_self_loops(chunk + 1)
+            if q == 2 and chunk + 1 < CHUNKS:
+                invert_sums(chunk + 1)
+            for b in range(B):
+                if step == h_start[b] + 9:
+                    quantise_h(b)

@@ -25,15 +25,14 @@ RUN = P // QUAD
 CHUNK = 4
 CHUNKS = ROWS // CHUNK
 ADJ_BUFS = 8
-SCALAR_SUMS = [1, 5, 7, 9, 11] + [i for i in range(24, ROWS) if i % 2 == 1]
-TENSOR_SUMS = (5, 7, 9, 11)
+SCALAR_SUMS = [i for i in range(ROWS) if i % 2 == 1 and not 12 <= i < 28]
 LEAD_VECTOR_SUM = 8
 LEAD_SCALAR_SUM = 10
 LAG_TRANSPOSE = 5
-LAG_COPY = 7
-H_READY = 24
+LAG_COPY = 6
+H_READY = 26
 QUANTISE_AT = [CHUNK * c + 13 for c in range(CHUNKS)]
-MULTIPLY_AT = [max(CHUNK * c + 14, H_READY + 2 * c) for c in range(CHUNKS)]
+MULTIPLY_AT = [max(CHUNK * c + 17, H_READY + 2 * c) for c in range(CHUNKS)]
 OUTPUT_AT = [step + 4 for step in MULTIPLY_AT]
 STEPS = OUTPUT_AT[-1] + 1
 
@@ -75,6 +74,11 @@ def tile_spconvlayer_kernel(tc, x, adj, weight, bias, out):
             in_=identity[:].rearrange("p (n b) -> p n b", b=QUAD),
             axis=mybir.AxisListType.X,
             op=ALU.add,
+        )
+        loops_by_pair = const.tile([P, 2, RUN // 2], F32)
+        nc.vector.tensor_copy(
+            out=loops_by_pair[:].rearrange("p e (j v) -> p e j v", v=2),
+            in_=loops[:].rearrange("p (j e v) -> p e j v", e=2, v=2),
         )
         ones = const.tile([P, P], BF16)
         nc.gpsimd.memset(ones[:], 1.0)
@@ -131,10 +135,13 @@ def tile_spconvlayer_kernel(tc, x, adj, weight, bias, out):
             chunk, q = divmod(i, CHUNK)
             return adj_sb[chunk][:, q * N : (q + 1) * N]
 
-        def on_diagonal(tile, chunk):
+        def on_diagonal(chunk, e):
             start = chunk * P % N
-            wide = tile[:, start : start + CHUNK * (N + RUN)]
-            return wide.rearrange("p (q c) -> p q c", c=N + RUN)[:, :, 0:RUN]
+            wide = adj_sb[chunk][:, start : start + CHUNK * (N + RUN)].rearrange("p (q c) -> p q c", c=N + RUN)
+            return wide[:, :, 0:RUN].rearrange("p q (j e v) -> p q e j v", e=2, v=2)[:, :, e, :, :]
+
+        def by_pair(values):
+            return values.rearrange("p (e j v) -> p e j v", e=2, v=2)
 
         def vector_lead(step):
             return min(LEAD_VECTOR_SUM, CHUNK + step // 2) if step >= 0 else CHUNK
@@ -157,32 +164,23 @@ def tile_spconvlayer_kernel(tc, x, adj, weight, bias, out):
                     op1=ALU.add,
                     accum_out=total,
                 )
-            elif i in TENSOR_SUMS:
-                bank = turn_psum.tile([P, P], F32, tag="turn", name="sum_bank")
-                for j in range(NB):
-                    nc.tensor.matmul(
-                        bank[:],
-                        lhsT=identity[:],
-                        rhs=row(i)[:, j * P : (j + 1) * P],
-                        start=(j == 0),
-                        stop=(j == NB - 1),
-                    )
-                nc.scalar.activation(
-                    out=unused_scalar[:, 0:P], in_=bank[:], func=ACT.Copy, bias=1.0 / P, accum_out=total
-                )
             else:
                 nc.scalar.activation(
                     out=unused_scalar[:], in_=row(i), func=ACT.Copy, bias=1.0 / N, accum_out=total
                 )
 
         def add_self_loops(chunk):
-            with_loops[chunk] = norm_pool.tile([P, CHUNK, RUN], F32, name="with_loops")
-            nc.vector.tensor_tensor(
-                out=with_loops[chunk][:],
-                in0=on_diagonal(adj_sb[chunk], chunk),
-                in1=loops[:].unsqueeze(1).to_broadcast([P, CHUNK, RUN]),
-                op=ALU.add,
-            )
+            with_loops[chunk] = norm_pool.tile([P, CHUNK, 2, RUN // 2], F32, name="with_loops")
+            for e in range(2):
+                nc.vector.tensor_tensor(
+                    out=with_loops[chunk][:, :, e, :].rearrange("p q (j v) -> p q j v", v=2),
+                    in0=on_diagonal(chunk, e),
+                    in1=loops_by_pair[:, e, :]
+                    .rearrange("p (j v) -> p j v", v=2)
+                    .unsqueeze(1)
+                    .to_broadcast([P, CHUNK, RUN // 4, 2]),
+                    op=ALU.add,
+                )
 
         def invert_sums(chunk):
             r[chunk] = norm_pool.tile([P, CHUNK], F32, name="r")
@@ -193,18 +191,21 @@ def tile_spconvlayer_kernel(tc, x, adj, weight, bias, out):
             if q == 0:
                 scaled[chunk] = scaled_pool.tile([P, (CHUNK + 1) * N], BF16, name="scaled")
             nc.vector.tensor_scalar(
-                out=scaled[chunk][:, q * N : (q + 1) * N],
-                in0=row(i),
+                out=by_pair(scaled[chunk][:, q * N : (q + 1) * N]),
+                in0=row(i).rearrange("p (j e v) -> p e j v", e=2, v=2),
                 scalar1=r[chunk][:, q : q + 1],
                 scalar2=None,
                 op0=ALU.mult,
             )
 
         def scale_diagonal(chunk):
+            start = chunk * P % N // 2
+            wide = scaled[chunk][:, start : start + CHUNK * (N + RUN // 2)]
+            rows = wide.rearrange("p (q c) -> p q c", c=N + RUN // 2)
             nc.vector.tensor_tensor(
-                out=on_diagonal(scaled[chunk], chunk),
+                out=rows[:, :, 0:N].rearrange("p q (e c) -> p q e c", e=2)[:, :, :, 0 : RUN // 2],
                 in0=with_loops[chunk][:],
-                in1=r[chunk][:].unsqueeze(2).to_broadcast([P, CHUNK, RUN]),
+                in1=r[chunk][:].unsqueeze(2).unsqueeze(3).to_broadcast([P, CHUNK, 2, RUN // 2]),
                 op=ALU.mult,
             )
 
@@ -214,7 +215,8 @@ def tile_spconvlayer_kernel(tc, x, adj, weight, bias, out):
             pairs = scaled[chunk][:, q * N : (q + 1) * N].bitcast(F32)
             for g in range(PASSES):
                 for e in range(2):
-                    source = pairs[:, 2 * P * g + e : 2 * P * (g + 1) : 2]
+                    first = (e * PASSES + g) * P
+                    source = pairs[:, first : first + P]
                     nc.tensor.transpose(turned[i][:, e, g, :], source, permutation[:])
 
         def copy_rows(i):
@@ -291,15 +293,15 @@ def tile_spconvlayer_kernel(tc, x, adj, weight, bias, out):
                 in_=h_grouped[b][:].rearrange("p g f t -> p (g f t)"),
             )
 
-        load_adj(0, 0, 2)
-        load_adj(0, 2, 4)
+        load_adj(0, 0, 1)
+        load_adj(0, 1, 4)
         load_adj(1, 0, 4)
+        load_adj(2, 0, 4)
         load_constants()
         load_x(0)
-        load_x(1)
-        load_adj(2, 0, 4)
-        load_x(2)
         load_adj(3, 0, 4)
+        load_x(1)
+        load_x(2)
         load_x(3)
         for chunk in range(4, ADJ_BUFS):
             load_adj(chunk, 0, CHUNK)
@@ -314,7 +316,7 @@ def tile_spconvlayer_kernel(tc, x, adj, weight, bias, out):
             if i in SCALAR_SUMS:
                 sum_rows(i)
 
-        h_start = [3 * b if b < QUAD else 14 + 6 * (b - QUAD) for b in range(B)]
+        h_start = [3 * b + 5 if b < QUAD else 18 + 5 * (b - QUAD) for b in range(B)]
 
         for step in range(STEPS):
             chunk, q = divmod(step, CHUNK)

@@ -25,7 +25,7 @@ RUN = P // QUAD
 CHUNK = 4
 CHUNKS = ROWS // CHUNK
 ADJ_BUFS = 8
-SCALAR_SUMS = [i for i in range(ROWS) if i % 2 == 1 and not 12 <= i < 28]
+SCALAR_SUMS = [i for i in range(ROWS) if i % 2 == 1 and i != 3 and not 12 <= i < 28]
 LEAD_VECTOR_SUM = 8
 LEAD_SCALAR_SUM = 10
 LAG_TRANSPOSE = 5
@@ -172,7 +172,7 @@ def tile_spconvlayer_kernel(tc, x, adj, weight, bias, out):
         def add_self_loops(chunk):
             with_loops[chunk] = norm_pool.tile([P, CHUNK, 2, RUN // 2], F32, name="with_loops")
             for e in range(2):
-                nc.vector.tensor_tensor(
+                nc.gpsimd.tensor_tensor(
                     out=with_loops[chunk][:, :, e, :].rearrange("p q (j v) -> p q j v", v=2),
                     in0=on_diagonal(chunk, e),
                     in1=loops_by_pair[:, e, :]
@@ -229,18 +229,29 @@ def tile_spconvlayer_kernel(tc, x, adj, weight, bias, out):
                 in_=turned[i][:].rearrange("p e g (b n) -> p (g b) n e", b=QUAD),
             )
 
-        def quantise_chunk(chunk):
-            width = QUAD * PASSES * P
-            codes[chunk] = codes_pool.tile([P, width], U32, align_bytes=64, name="codes")
-            scales[chunk] = codes_pool.tile([P, width], U8, align_bytes=64, name="scales")
-            nc.vector.quantize_mx(
-                out=codes[chunk][:].bitcast(FP8X4), scales=scales[chunk][:], in_=grouped[chunk][:]
-            )
+        def parts_of(chunk):
+            return [(0, QUAD)] if chunk < CHUNKS - 1 else [(0, 2), (2, QUAD)]
 
-        def multiply_chunk(chunk):
+        def quantise_part(chunk, first, last):
+            if first == 0:
+                width = QUAD * PASSES * P
+                codes[chunk] = codes_pool.tile([P, width], U32, align_bytes=64, name="codes")
+                scales[chunk] = codes_pool.tile([P, width], U8, align_bytes=64, name="scales")
+            pieces = [(0, QUAD * PASSES)]
+            if last - first < QUAD:
+                pieces = [(g * QUAD + first, g * QUAD + last) for g in range(PASSES)]
+            for lo, hi in pieces:
+                nc.vector.quantize_mx(
+                    out=codes[chunk][:, lo * P : hi * P].bitcast(FP8X4),
+                    scales=scales[chunk][:, lo * P : hi * P],
+                    in_=grouped[chunk][:, lo * P * 4 : hi * P * 4],
+                )
+
+        def multiply_part(chunk, first, last):
             d = chunk // (CHUNKS * QUAD // B)
-            product[chunk] = product_psum.tile([P, QUAD, F], F32, name="product")
-            for b in range(QUAD):
+            if first == 0:
+                product[chunk] = product_psum.tile([P, QUAD, F], F32, name="product")
+            for b in range(first, last):
                 for g in range(PASSES):
                     a_cols = slice((g * QUAD + b) * P, (g * QUAD + b + 1) * P)
                     h_first = ((QUAD * d + b) * PASSES + g) * F
@@ -255,18 +266,18 @@ def tile_spconvlayer_kernel(tc, x, adj, weight, bias, out):
                         stop=(g == PASSES - 1),
                     )
 
-        def output_chunk(chunk):
+        def output_part(chunk, first, last):
             d, part = divmod(chunk, CHUNKS * QUAD // B)
-            result = result_pool.tile([P, QUAD, F], F32, name="result")
+            result = result_pool.tile([P, last - first, F], F32, name="result")
             nc.vector.scalar_tensor_tensor(
                 out=result[:],
-                in0=product[chunk][:],
+                in0=product[chunk][:, first:last, :],
                 scalar=0.0,
-                in1=bias_f32[:].unsqueeze(1).to_broadcast([P, QUAD, F]),
+                in1=bias_f32[:].unsqueeze(1).to_broadcast([P, last - first, F]),
                 op0=ALU.max,
                 op1=ALU.add,
             )
-            nc.sync.dma_start(out=out_view[d][part], in_=result[:])
+            nc.sync.dma_start(out=out_view[d][part][:, first:last, :], in_=result[:])
 
         def transpose_x(b):
             bank = turn_psum.tile([P, NB, P], BF16, tag="turn", name="x_bank")
@@ -322,10 +333,12 @@ def tile_spconvlayer_kernel(tc, x, adj, weight, bias, out):
             chunk, q = divmod(step, CHUNK)
             for c in range(CHUNKS):
                 if step == OUTPUT_AT[c]:
-                    output_chunk(c)
+                    for first, last in parts_of(c):
+                        output_part(c, first, last)
             for c in range(CHUNKS):
                 if step == MULTIPLY_AT[c]:
-                    multiply_chunk(c)
+                    for first, last in parts_of(c):
+                        multiply_part(c, first, last)
             if step < ROWS:
                 scale_rows(step)
             if q == 0 and 1 <= chunk <= CHUNKS:
@@ -338,7 +351,8 @@ def tile_spconvlayer_kernel(tc, x, adj, weight, bias, out):
                 copy_rows(step - LAG_COPY)
             for c in range(CHUNKS):
                 if step == QUANTISE_AT[c]:
-                    quantise_chunk(c)
+                    for first, last in parts_of(c):
+                        quantise_part(c, first, last)
             if step == 1:
                 spread_bias()
             for b in range(B):

from contextlib import ExitStack

import concourse.mybir as mybir
from concourse.masks import make_identity

BF16 = mybir.dt.bfloat16
F32 = mybir.dt.float32
U32 = mybir.dt.uint32
U8 = mybir.dt.uint8
FP8X4 = mybir.dt.float8_e4m3fn_x4
ALU = mybir.AluOpType
ACT = mybir.ActivationFunctionType

B = 8
N = 1024
F = 128
P = 128
NB = N // P
ROWS = B * NB
PASSES = N // (4 * P)
FLOPS = 2 * B * N * N * F + 2 * B * N * F * F

QUAD = 4
RUN = P // QUAD
CHUNK = 4
CHUNKS = ROWS // CHUNK
ADJ_BUFS = 8
SCALAR_SUMS = [i for i in range(ROWS) if i % 2 == 1 and i != 3 and not 12 <= i < 28]
LEAD_VECTOR_SUM = 8
LEAD_SCALAR_SUM = 10
LAG_TRANSPOSE = 5
LAG_COPY = 6
H_READY = 26
QUANTISE_AT = [CHUNK * c + 13 for c in range(CHUNKS)]
MULTIPLY_AT = [max(CHUNK * c + 17, H_READY + 2 * c) for c in range(CHUNKS)]
OUTPUT_AT = [step + 4 for step in MULTIPLY_AT]
STEPS = OUTPUT_AT[-1] + 1

def tile_spconvlayer_kernel(tc, x, adj, weight, bias, out):
    nc = tc.nc
    with ExitStack() as ctx:
        const = ctx.enter_context(tc.tile_pool(name="const", bufs=1))
        adj_pool = ctx.enter_context(tc.tile_pool(name="adj_pool", bufs=ADJ_BUFS))
        norm_pool = ctx.enter_context(tc.tile_pool(name="norm_pool", bufs=6))
        scaled_pool = ctx.enter_context(tc.tile_pool(name="scaled_pool", bufs=3))
        words_pool = ctx.enter_context(tc.tile_pool(name="words_pool", bufs=4))
        codes_pool = ctx.enter_context(tc.tile_pool(name="codes_pool", bufs=6))
        result_pool = ctx.enter_context(tc.tile_pool(name="result_pool", bufs=4))
        h_pool = ctx.enter_context(tc.tile_pool(name="h_pool", bufs=2))
        turn_psum = ctx.enter_context(tc.psum_pool(name="turn_psum", bufs=6))
        product_psum = ctx.enter_context(tc.psum_pool(name="product_psum", bufs=2))
        ctx.enter_context(tc.manual_schedule())

        x_view = x.rearrange("b (g p t) m a -> b p g (t m a)", p=P, t=4)
        adj_view = adj.rearrange("b (s q n) c -> b s n q c", q=CHUNK, n=RUN)
        out_view = out.rearrange("(d b) (s p) u w -> d s p b (u w)", b=QUAD, p=P)

        warm = const.tile([P, 2], F32)
        nc.vector.memset(warm[:], 0.0)
        nc.scalar.activation(out=warm[:, 0:1], in_=warm[:, 1:2], func=ACT.Copy)

        identity = const.tile([P, P], BF16)
        make_identity(nc, identity[:])
        identity_f32 = const.tile([P, P], F32)
        make_identity(nc, identity_f32[:])
        permutation = const.tile([P, P], F32)
        nc.vector.tensor_copy(
            out=permutation[:].rearrange("p (b n) -> p b n", b=QUAD),
            in_=identity_f32[:].rearrange("p (n b) -> p b n", b=QUAD),
        )
        loops = const.tile([P, RUN], F32)
        nc.vector.tensor_reduce(
            out=loops[:],
            in_=identity[:].rearrange("p (n b) -> p n b", b=QUAD),
            axis=mybir.AxisListType.X,
            op=ALU.add,
        )
        loops_by_pair = const.tile([P, 2, RUN // 2], F32)
        nc.vector.tensor_copy(
            out=loops_by_pair[:].rearrange("p e (j v) -> p e j v", v=2),
            in_=loops[:].rearrange("p (j e v) -> p e j v", e=2, v=2),
        )
        ones = const.tile([P, P], BF16)
        nc.gpsimd.memset(ones[:], 1.0)
        bias_row = const.tile([P, F], BF16)
        nc.gpsimd.memset(bias_row[:], 0.0)
        w_sb = const.tile([P, F], BF16)
        bias_f32 = const.tile([P, F], F32)
        x_sb = const.tile([P, B, PASSES, 4 * F], BF16)
        h_codes = const.tile([P, B * PASSES * F], U32, align_bytes=64)
        h_scales = const.tile([P, B * PASSES * F], U8, align_bytes=64)
        unused_vector = const.tile([P, N], BF16)
        unused_scalar = const.tile([P, N], BF16)

        adj_sb = {}
        sums = {}
        r = {}
        with_loops = {}
        scaled = {}
        grouped = {}
        codes = {}
        scales = {}
        product = {}
        x_turned = {}
        h_grouped = {}
        turned = {}

        def load_adj(chunk, lo, hi):
            if chunk not in adj_sb:
                adj_sb[chunk] = adj_pool.tile([P, (CHUNK + 1) * N], BF16, name="adj_sb")
            rows = adj_sb[chunk][:, 0 : CHUNK * N].rearrange("p (q c) -> p q c", c=N)
            d, part = divmod(chunk, CHUNKS * QUAD // B)
            for b in range(QUAD):
                nc.sync.dma_start(
                    out=rows[b:P:QUAD, lo:hi, :], in_=adj_view[QUAD * d + b][part][:, lo:hi, :]
                )

        def load_x(b):
            nc.sync.dma_start(out=x_sb[:, b, :, :], in_=x_view[b])

        def load_constants():
            for m in range(4):
                nc.sync.dma_start(
                    out=w_sb[32 * m : 32 * m + 32, :].rearrange("a (u w) -> a u w", u=4),
                    in_=weight[m].rearrange("u a w -> a u w"),
                )
            nc.sync.dma_start(out=bias_row[0:1, :], in_=bias.rearrange("o i u w -> (o i) (u w)"))

        def spread_bias():
            bank = turn_psum.tile([P, F], F32, tag="turn", name="bias_bank")
            nc.tensor.matmul(bank[:], lhsT=ones[:], rhs=bias_row[:], start=True, stop=True)
            nc.scalar.copy(out=bias_f32[:], in_=bank[:])

        def row(i):
            chunk, q = divmod(i, CHUNK)
            return adj_sb[chunk][:, q * N : (q + 1) * N]

        def on_diagonal(chunk, e):
            start = chunk * P % N
            wide = adj_sb[chunk][:, start : start + CHUNK * (N + RUN)].rearrange("p (q c) -> p q c", c=N + RUN)
            return wide[:, :, 0:RUN].rearrange("p q (j e v) -> p q e j v", e=2, v=2)[:, :, e, :, :]

        def by_pair(values):
            return values.rearrange("p (e j v) -> p e j v", e=2, v=2)

        def vector_lead(step):
            return min(LEAD_VECTOR_SUM, CHUNK + step // 2) if step >= 0 else CHUNK

        def scalar_lead(step):
            return min(LEAD_SCALAR_SUM, 2 * CHUNK + 2 * step)

        def sum_rows(i):
            chunk, q = divmod(i, CHUNK)
            if chunk not in sums:
                sums[chunk] = norm_pool.tile([P, CHUNK], F32, name="sums")
            total = sums[chunk][:, q : q + 1]
            if i not in SCALAR_SUMS:
                nc.vector.tensor_scalar(
                    out=unused_vector[:],
                    in0=row(i),
                    scalar1=1.0,
                    scalar2=1.0,
                    op0=ALU.mult,
                    op1=ALU.add,
                    accum_out=total,
                )
            else:
                nc.scalar.activation(
                    out=unused_scalar[:], in_=row(i), func=ACT.Copy, bias=1.0 / N, accum_out=total
                )

        def add_self_loops(chunk):
            with_loops[chunk] = norm_pool.tile([P, CHUNK, 2, RUN // 2], F32, name="with_loops")
            for e in range(2):
                nc.gpsimd.tensor_tensor(
                    out=with_loops[chunk][:, :, e, :].rearrange("p q (j v) -> p q j v", v=2),
                    in0=on_diagonal(chunk, e),
                    in1=loops_by_pair[:, e, :]
                    .rearrange("p (j v) -> p j v", v=2)
                    .unsqueeze(1)
                    .to_broadcast([P, CHUNK, RUN // 4, 2]),
                    op=ALU.add,
                )

        def invert_sums(chunk):
            r[chunk] = norm_pool.tile([P, CHUNK], F32, name="r")
            nc.vector.reciprocal(r[chunk][:], sums[chunk][:])

        def scale_rows(i):
            chunk, q = divmod(i, CHUNK)
            if q == 0:
                scaled[chunk] = scaled_pool.tile([P, (CHUNK + 1) * N], BF16, name="scaled")
            nc.vector.tensor_scalar(
                out=by_pair(scaled[chunk][:, q * N : (q + 1) * N]),
                in0=row(i).rearrange("p (j e v) -> p e j v", e=2, v=2),
                scalar1=r[chunk][:, q : q + 1],
                scalar2=None,
                op0=ALU.mult,
            )

        def scale_diagonal(chunk):
            start = chunk * P % N // 2
            wide = scaled[chunk][:, start : start + CHUNK * (N + RUN // 2)]
            rows = wide.rearrange("p (q c) -> p q c", c=N + RUN // 2)
            nc.vector.tensor_tensor(
                out=rows[:, :, 0:N].rearrange("p q (e c) -> p q e c", e=2)[:, :, :, 0 : RUN // 2],
                in0=with_loops[chunk][:],
                in1=r[chunk][:].unsqueeze(2).unsqueeze(3).to_broadcast([P, CHUNK, 2, RUN // 2]),
                op=ALU.mult,
            )

        def transpose_rows(i):
            chunk, q = divmod(i, CHUNK)
            turned[i] = turn_psum.tile([P, 2, PASSES, P], F32, tag="turn", name="turned")
            pairs = scaled[chunk][:, q * N : (q + 1) * N].bitcast(F32)
            for g in range(PASSES):
                for e in range(2):
                    first = (e * PASSES + g) * P
                    source = pairs[:, first : first + P]
                    nc.tensor.transpose(turned[i][:, e, g, :], source, permutation[:])

        def copy_rows(i):
            chunk, q = divmod(i, CHUNK)
            if q == 0:
                grouped[chunk] = words_pool.tile([P, CHUNK * N], BF16, align_bytes=64, name="grouped")
            words = grouped[chunk][:].bitcast(F32).rearrange("p (k n e) -> p k n e", n=P, e=2)
            nc.scalar.copy(
                out=words[:, :, q * RUN : (q + 1) * RUN, :],
                in_=turned[i][:].rearrange("p e g (b n) -> p (g b) n e", b=QUAD),
            )

        def parts_of(chunk):
            return [(0, QUAD)] if chunk < CHUNKS - 1 else [(0, 2), (2, QUAD)]

        def quantise_part(chunk, first, last):
            if first == 0:
                width = QUAD * PASSES * P
                codes[chunk] = codes_pool.tile([P, width], U32, align_bytes=64, name="codes")
                scales[chunk] = codes_pool.tile([P, width], U8, align_bytes=64, name="scales")
            pieces = [(0, QUAD * PASSES)]
            if last - first < QUAD:
                pieces = [(g * QUAD + first, g * QUAD + last) for g in range(PASSES)]
            for lo, hi in pieces:
                nc.vector.quantize_mx(
                    out=codes[chunk][:, lo * P : hi * P].bitcast(FP8X4),
                    scales=scales[chunk][:, lo * P : hi * P],
                    in_=grouped[chunk][:, lo * P * 4 : hi * P * 4],
                )

        def multiply_part(chunk, first, last):
            d = chunk // (CHUNKS * QUAD // B)
            if first == 0:
                product[chunk] = product_psum.tile([P, QUAD, F], F32, name="product")
            for b in range(first, last):
                for g in range(PASSES):
                    a_cols = slice((g * QUAD + b) * P, (g * QUAD + b + 1) * P)
                    h_first = ((QUAD * d + b) * PASSES + g) * F
                    h_cols = slice(h_first, h_first + F)
                    nc.tensor.matmul_mx(
                        out=product[chunk][:, b, :],
                        lhsT=codes[chunk][:, a_cols].bitcast(FP8X4),
                        lhsT_scale=scales[chunk][:, a_cols],
                        rhs=h_codes[:, h_cols].bitcast(FP8X4),
                        rhs_scale=h_scales[:, h_cols],
                        start=(g == 0),
                        stop=(g == PASSES - 1),
                    )

        def output_part(chunk, first, last):
            d, part = divmod(chunk, CHUNKS * QUAD // B)
            result = result_pool.tile([P, last - first, F], F32, name="result")
            nc.vector.scalar_tensor_tensor(
                out=result[:],
                in0=product[chunk][:, first:last, :],
                scalar=0.0,
                in1=bias_f32[:].unsqueeze(1).to_broadcast([P, last - first, F]),
                op0=ALU.max,
                op1=ALU.add,
            )
            nc.sync.dma_start(out=out_view[d][part][:, first:last, :], in_=result[:])

        def transpose_x(b):
            bank = turn_psum.tile([P, NB, P], BF16, tag="turn", name="x_bank")
            for j in range(NB):
                nc.tensor.transpose(bank[:, j, :], x_sb[:, b, j // 4, (j % 4) * F : (j % 4 + 1) * F], identity[:])
            x_turned[b] = h_pool.tile([P, NB, P], BF16, name="x_turned")
            nc.scalar.copy(out=x_turned[b][:], in_=bank[:])

        def multiply_x(b, g):
            if g == 0:
                h_grouped[b] = h_pool.tile([P, PASSES, F, 4], BF16, align_bytes=64, name="h_grouped")
            bank = turn_psum.tile([P, 4, F], F32, tag="turn", name="h_bank")
            for t in range(4):
                nc.tensor.matmul(
                    bank[:, t, :], lhsT=x_turned[b][:, 4 * g + t, :], rhs=w_sb[:], start=True, stop=True
                )
            nc.scalar.copy(out=h_grouped[b][:, g, :, :], in_=bank[:].rearrange("p t f -> p f t"))

        def quantise_h(b):
            cols = slice(b * PASSES * F, (b + 1) * PASSES * F)
            nc.vector.quantize_mx(
                out=h_codes[:, cols].bitcast(FP8X4),
                scales=h_scales[:, cols],
                in_=h_grouped[b][:].rearrange("p g f t -> p (g f t)"),
            )

        load_adj(0, 0, 1)
        load_adj(0, 1, 4)
        load_adj(1, 0, 4)
        load_adj(2, 0, 4)
        load_constants()
        load_x(0)
        load_adj(3, 0, 4)
        load_x(1)
        load_x(2)
        load_x(3)
        for chunk in range(4, ADJ_BUFS):
            load_adj(chunk, 0, CHUNK)
        for b in range(4, B):
            load_x(b)

        for i in range(CHUNK):
            sum_rows(i)
        invert_sums(0)
        add_self_loops(0)
        for i in range(CHUNK, 2 * CHUNK):
            if i in SCALAR_SUMS:
                sum_rows(i)

        h_start = [3 * b + 5 if b < QUAD else 18 + 5 * (b - QUAD) for b in range(B)]

        for step in range(STEPS):
            chunk, q = divmod(step, CHUNK)
            for c in range(CHUNKS):
                if step == OUTPUT_AT[c]:
                    for first, last in parts_of(c):
                        output_part(c, first, last)
            for c in range(CHUNKS):
                if step == MULTIPLY_AT[c]:
                    for first, last in parts_of(c):
                        multiply_part(c, first, last)
            if step < ROWS:
                scale_rows(step)
            if q == 0 and 1 <= chunk <= CHUNKS:
                scale_diagonal(chunk - 1)
            if q == CHUNK - 1 and chunk + ADJ_BUFS < CHUNKS:
                load_adj(chunk + ADJ_BUFS, 0, CHUNK)
            if 0 <= step - LAG_TRANSPOSE < ROWS:
                transpose_rows(step - LAG_TRANSPOSE)
            if 0 <= step - LAG_COPY < ROWS:
                copy_rows(step - LAG_COPY)
            for c in range(CHUNKS):
                if step == QUANTISE_AT[c]:
                    for first, last in parts_of(c):
                        quantise_part(c, first, last)
            if step == 1:
                spread_bias()
            for b in range(B):
                if step == h_start[b]:
                    transpose_x(b)
                if step == h_start[b] + 1:
                    multiply_x(b, 0)
                if step == h_start[b] + 2:
                    multiply_x(b, 1)
            for i in range(vector_lead(step - 1) + step, min(vector_lead(step) + step + 1, ROWS)):
                if i not in SCALAR_SUMS:
                    sum_rows(i)
            for i in range(2 * CHUNK if step == 0 else step + scalar_lead(step - 1), step + scalar_lead(step) + 1):
                if i in SCALAR_SUMS:
                    sum_rows(i)
            if q == 1 and chunk + 1 < CHUNKS:
                add_self_loops(chunk + 1)
            if q == 2 and chunk + 1 < CHUNKS:
                invert_sums(chunk + 1)
            for b in range(B):
                if step == h_start[b] + 9:
                    quantise_h(b)
